import numpy as np
import ml_dtypes


def mxq(x, axis, fmt="e4m3"):
    dtype, down = {"e4m3": (ml_dtypes.float8_e4m3fn, 7), "e5m2": (ml_dtypes.float8_e5m2, 14)}[fmt]
    v = np.moveaxis(np.asarray(x, np.float32).astype(ml_dtypes.bfloat16).astype(np.float64), axis, -1)
    blocks = v.reshape(v.shape[:-1] + (-1, 32))
    amax = np.abs(blocks).max(-1, keepdims=True)
    byte = np.maximum(np.where(amax > 0, np.frexp(amax)[1] - 1 + 127, 0) - down, 1)
    scale = np.exp2(byte - 127.0)
    codes = (blocks / scale).astype(np.float32).astype(dtype).astype(np.float64)
    return np.moveaxis((codes * scale).reshape(v.shape), -1, axis)


WIDE = False


def mx_kscale(k):
    if not WIDE:
        return np.ones(k)
    levels = np.array([10, -10, 5, -5, 0])
    if k % 512:
        return np.exp2(np.random.permutation(np.resize(levels, k // 32))).repeat(32)
    a = np.empty((k // 512, 16))
    for p in range(k // 512):
        a[p, :8] = np.random.permutation(np.resize(levels, 8))
        for g in range(8):
            far = levels[np.abs(levels - a[p, g]) >= 10]
            a[p, g + 8] = far[np.random.randint(len(far))]
    return np.exp2(a.ravel()).repeat(32)


BF16 = ml_dtypes.bfloat16


def bf(x):
    return np.asarray(x, np.float32).astype(BF16)


def f64(x):
    return np.asarray(x).astype(np.float64)


B, N, C, DIM, H = 2, 64, 1024, 1024, 16
D = DIM // H // 2
LAYER_NUM = 12
LAM_INIT = 0.8 - 0.6 * np.exp(-0.3 * LAYER_NUM)
SCALE = D ** -0.5


def split_qk(y):
    y = y.reshape(B, N, H, D, 2)
    return np.moveaxis(y, -1, 2).reshape(B, N, 2 * H, D)


def setup_inputs():
    s = mx_kscale(C)
    ls = 0.45 / D ** 0.25
    return {"x": bf(np.random.standard_normal((B, N, C)) * s),
            "Wq": bf(np.random.standard_normal((DIM, C)) / np.sqrt(C) / s),
            "Wk": bf(np.random.standard_normal((DIM, C)) / np.sqrt(C) / s),
            "lq1": bf(np.random.standard_normal(D) * ls),
            "lq2": bf(np.random.standard_normal(D) * ls),
            "lk1": bf(np.random.standard_normal(D) * ls),
            "lk2": bf(np.random.standard_normal(D) * ls)}


def reference(x, Wq, Wk, lq1, lq2, lk1, lk2):
    xq = mxq(f64(x), 2, "e4m3")
    q = split_qk(xq @ mxq(f64(Wq), 1, "e4m3").T) * SCALE
    k = split_qk(xq @ mxq(f64(Wk), 1, "e4m3").T)
    sc = np.stack([(q[:, :, i:i + 1, :] * k).sum(-1) for i in range(2 * H)], axis=2)
    e = np.exp(sc - sc.max(-1, keepdims=True))
    att = e / e.sum(-1, keepdims=True)
    lam = np.exp(np.sum(f64(lq1) * f64(lk1))) - np.exp(np.sum(f64(lq2) * f64(lk2))) + LAM_INIT
    return att[:, :, :H, :H] - lam * att[:, :, H:, H:]

@@ -1,0 +1,292 @@
+from contextlib import ExitStack
+import math
+
+import concourse.mybir as mybir
+from concourse.masks import make_identity
+
+F32 = mybir.dt.float32
+BF16 = mybir.dt.bfloat16
+U32 = mybir.dt.uint32
+U8 = mybir.dt.uint8
+I32 = mybir.dt.int32
+FP8X4 = mybir.dt.float8_e4m3fn_x4
+ALU = mybir.AluOpType
+ACT = mybir.ActivationFunctionType
+AXIS = mybir.AxisListType
+
+P = 128
+K = 1024
+K_PASS = 512
+PASSES = K // K_PASS
+WORDS = K // 2
+HEADS = 16
+ROWS = 2 * HEADS
+D = 32
+QUAD = 32
+QUADS = P // QUAD
+BANK = 512
+W_TILES = 4
+PAIRS = 4
+PAIR_HEADS = 8
+CHUNK = 8
+CHUNKS = QUAD // CHUNK
+SCALE = D ** -0.5
+LAM_INIT = 0.8 - 0.6 * math.exp(-0.3 * 12)
+BURST = 16
+SCORE_COLS = 44
+
+FLOPS = 2 * P * K * 2 * K + 2 * P * ROWS * ROWS * D
+
+
+def regroup_rows(nc, banks, ident, row_words, grouped_words):
+    bank = banks.tile([P, 2 * PASSES, P], F32, tag="bank", name="bank")
+    for g in range(PASSES):
+        for u in range(2):
+            every_2nd = slice(2 * P * g + u, 2 * P * (g + 1), 2)
+            nc.tensor.transpose(bank[:, 2 * g + u, :], row_words[:, every_2nd], ident)
+    nc.scalar.copy(
+        out=grouped_words.rearrange("p (g r u) -> p g r u", g=PASSES, u=2),
+        in_=bank[:].rearrange("p (g u) r -> p g r u", u=2),
+    )
+
+
+def tile_differentialattention_pa_s_kernel(tc, x, Wq, Wk, lq1, lq2, lk1, lk2, out):
+    nc = tc.nc
+    with ExitStack() as ctx:
+        keep = ctx.enter_context(tc.tile_pool(name="keep", bufs=1))
+        stage = ctx.enter_context(tc.tile_pool(name="stage", bufs=4))
+        banks = ctx.enter_context(tc.psum_pool(name="banks", bufs=5))
+        y_pool = ctx.enter_context(tc.psum_pool(name="y_pool", bufs=2))
+        idle_pool = ctx.enter_context(tc.psum_pool(name="idle_pool", bufs=1))
+        ctx.enter_context(tc.manual_schedule())
+
+        x_sb = keep.tile([P, K], BF16, name="x_sb")
+        nc.sync.dma_start(out=x_sb[:], in_=x.rearrange("b n k -> (b n) k"))
+        w_tiles = []
+        for w in (Wq, Wk):
+            w_view = w.rearrange("(s p j) k -> s p (j k)", p=P, j=2)
+            for s in range(W_TILES):
+                w_sb = keep.tile([P, 2 * K], BF16, name="w_sb%d" % len(w_tiles))
+                nc.sync.dma_start(out=w_sb[:], in_=w_view[s])
+                w_tiles.append(w_sb)
+
+        lam_rows = keep.tile([P, 4 * D], BF16, name="lam_rows")
+        nc.vector.memset(lam_rows[:], 0.0)
+        for n, vector in enumerate((lq1, lq2, lk1, lk2)):
+            nc.scalar.dma_start(
+                out=lam_rows[0:1, n * D : (n + 1) * D], in_=vector.rearrange("(o d) -> o d", o=1)
+            )
+
+        ident = keep.tile([P, P], F32, name="ident")
+        make_identity(nc, ident[:])
+        ones = keep.tile([P, P], BF16, name="ones")
+        nc.vector.memset(ones[:], 1.0)
+        warm = keep.tile([P, 2], F32, name="warm")
+        nc.vector.memset(warm[:], 0.0)
+        nc.scalar.activation(out=warm[:, 1:2], in_=warm[:, 0:1], func=ACT.Exp)
+        idle_zeros = keep.tile([P, 4 * P], BF16, align_bytes=64, name="idle_zeros")
+        idle_codes = keep.tile([P, P], U32, align_bytes=64, name="idle_codes")
+        idle_scales = keep.tile([P, P], U8, align_bytes=64, name="idle_scales")
+        nc.vector.memset(idle_zeros[:].bitcast(I32), 0)
+        nc.vector.quantize_mx(
+            out=idle_codes[:].bitcast(FP8X4), scales=idle_scales[:], in_=idle_zeros[:]
+        )
+        idle_bank = idle_pool.tile([P, P], F32, name="idle_bank")
+
+        def hold_clock(passes):
+            for repeat in range(passes):
+                nc.tensor.matmul_mx(
+                    out=idle_bank[:],
+                    lhsT=idle_codes[:].bitcast(FP8X4),
+                    lhsT_scale=idle_scales[:],
+                    rhs=idle_codes[:].bitcast(FP8X4),
+                    rhs_scale=idle_scales[:],
+                    start=True,
+                    stop=True,
+                )
+
+        q_blocks = keep.tile([P, QUAD, QUADS, ROWS], F32, name="q_blocks")
+        nc.vector.memset(q_blocks[:], 0.0)
+        k_cols = keep.tile([P, QUAD + 1, ROWS], F32, name="k_cols")
+        nc.vector.memset(k_cols[:, QUAD, :], 0.0)
+
+        x_grouped = keep.tile([P, PASSES * P * 4], BF16, align_bytes=64, name="x_grouped")
+        regroup_rows(nc, banks, ident[:], x_sb[:].bitcast(F32), x_grouped[:].bitcast(F32))
+        x_codes = keep.tile([P, PASSES * P], U32, align_bytes=64, name="x_codes")
+        x_scales = keep.tile([P, PASSES * P], U8, align_bytes=64, name="x_scales")
+        nc.vector.quantize_mx(out=x_codes[:].bitcast(FP8X4), scales=x_scales[:], in_=x_grouped[:])
+
+        grouped = {}
+        w_codes = {}
+        w_scales = {}
+
+        def regroup_tile(n):
+            grouped[n] = stage.tile([P, 2 * PASSES * P * 4], BF16, align_bytes=64, name="grouped")
+            for j in range(2):
+                words = slice(j * WORDS, (j + 1) * WORDS)
+                regroup_rows(
+                    nc,
+                    banks,
+                    ident[:],
+                    w_tiles[n][:].bitcast(F32)[:, words],
+                    grouped[n][:].bitcast(F32)[:, words],
+                )
+
+        def quantise_tile(n):
+            w_codes[n] = stage.tile([P, 2 * PASSES * P], U32, align_bytes=64, name="w_codes")
+            w_scales[n] = stage.tile([P, 2 * PASSES * P], U8, align_bytes=64, name="w_scales")
+            nc.vector.quantize_mx(
+                out=w_codes[n][:].bitcast(FP8X4), scales=w_scales[n][:], in_=grouped[n][:]
+            )
+
+        def multiply_tile(n, y_bank):
+            for j in range(2):
+                y_start = j * (BANK // 2) + (n % 2) * P
+                for g in range(PASSES):
+                    x_cols = slice(g * P, (g + 1) * P)
+                    w_cols = slice((j * PASSES + g) * P, (j * PASSES + g + 1) * P)
+                    nc.tensor.matmul_mx(
+                        out=y_bank[:, y_start : y_start + P],
+                        lhsT=x_codes[:, x_cols].bitcast(FP8X4),
+                        lhsT_scale=x_scales[:, x_cols],
+                        rhs=w_codes[n][:, w_cols].bitcast(FP8X4),
+                        rhs_scale=w_scales[n][:, w_cols],
+                        start=(g == 0),
+                        stop=(g == PASSES - 1),
+                    )
+
+        def unpack_bank(pair, y_bank):
+            swapped = stage.tile([P, BANK], F32, align_bytes=64, name="swapped")
+            nc.vector.transpose(out=swapped[:], in_=y_bank[:])
+            heads = slice((pair % 2) * PAIR_HEADS, (pair % 2 + 1) * PAIR_HEADS)
+            if pair < PAIRS // 2:
+                for c in range(QUADS):
+                    rows = slice(c * QUAD, (c + 1) * QUAD)
+                    source = swapped[rows, :].rearrange("p (j h t) -> p t j h", j=2, t=QUAD)
+                    target = q_blocks[rows, :, c, :].rearrange("p t (j h) -> p t j h", j=2)
+                    if c % 2 == 0:
+                        nc.vector.tensor_copy(out=target[:, :, :, heads], in_=source)
+                    else:
+                        nc.gpsimd.tensor_scalar(
+                            out=target[:, :, :, heads],
+                            in0=source,
+                            scalar1=1.0,
+                            scalar2=0.0,
+                            op0=ALU.mult,
+                            op1=ALU.add,
+                        )
+            else:
+                source = swapped[:].rearrange("p (j h t) -> p t j h", j=2, t=QUAD)
+                target = k_cols[:, 0:QUAD, :].rearrange("p t (j h) -> p t j h", j=2)
+                first = slice(0, QUAD // 2)
+                second = slice(QUAD // 2, QUAD)
+                nc.vector.tensor_copy(out=target[:, first, :, heads], in_=source[:, first])
+                nc.scalar.copy(out=target[:, second, :, heads], in_=source[:, second])
+
+        for weight in range(2):
+            tiles = range(weight * W_TILES, (weight + 1) * W_TILES)
+            for n in tiles:
+                regroup_tile(n)
+                if n > tiles[0]:
+                    quantise_tile(n - 1)
+            quantise_tile(tiles[-1])
+            for pair in (2 * weight, 2 * weight + 1):
+                y_bank = y_pool.tile([P, BANK], F32, tag="y_bank", name="y_bank")
+                multiply_tile(2 * pair, y_bank)
+                multiply_tile(2 * pair + 1, y_bank)
+                unpack_bank(pair, y_bank)
+        hold_clock(BURST)
+
+        lam_bank = banks.tile([P, 4 * D], F32, tag="bank", name="lam_bank")
+        nc.tensor.matmul(out=lam_bank[:], lhsT=ones[:], rhs=lam_rows[:], start=True, stop=True)
+        lam_all = keep.tile([P, 4 * D], F32, name="lam_all")
+        nc.scalar.copy(out=lam_all[:], in_=lam_bank[:])
+        lam_prod = keep.tile([P, 2, D], F32, name="lam_prod")
+        nc.vector.tensor_tensor(
+            out=lam_prod[:].rearrange("p n d -> p (n d)"),
+            in0=lam_all[:, 0 : 2 * D],
+            in1=lam_all[:, 2 * D : 4 * D],
+            op=ALU.mult,
+        )
+        lam_dots = keep.tile([P, 2], F32, name="lam_dots")
+        nc.vector.tensor_reduce(out=lam_dots[:], in_=lam_prod[:], axis=AXIS.X, op=ALU.add)
+        lam_exp = keep.tile([P, 2], F32, name="lam_exp")
+        nc.scalar.activation(out=lam_exp[:], in_=lam_dots[:], func=ACT.Exp)
+        neg_lam = keep.tile([P, 1], F32, name="neg_lam")
+        nc.vector.scalar_tensor_tensor(
+            out=neg_lam[:],
+            in0=lam_exp[:, 1:2],
+            scalar=-LAM_INIT,
+            in1=lam_exp[:, 0:1],
+            op0=ALU.add,
+            op1=ALU.subtract,
+        )
+
+        k_flat = k_cols[:].rearrange("p t m -> p (t m)")
+        scores = []
+        for chunk in range(CHUNKS):
+            scores.append(banks.tile([P, CHUNK, SCORE_COLS], F32, tag="bank", name="scores"))
+            for t in range(CHUNK):
+                first_col = (chunk * CHUNK + t) * ROWS
+                nc.tensor.matmul(
+                    out=scores[chunk][:, t, :],
+                    lhsT=q_blocks[:, chunk * CHUNK + t].rearrange("p c i -> p (c i)"),
+                    rhs=k_flat[:, first_col : first_col + SCORE_COLS],
+                    start=True,
+                    stop=True,
+                )
+
+        top = keep.tile([P, QUAD], F32, name="top")
+        expd = keep.tile([P, ROWS, QUAD], F32, align_bytes=64, name="expd")
+        sums = keep.tile([P, QUAD], F32, name="sums")
+        inverse = keep.tile([P, QUAD], F32, name="inverse")
+        for chunk in range(CHUNKS + 1):
+            ts = slice(chunk * CHUNK, (chunk + 1) * CHUNK)
+            done = slice((chunk - 1) * CHUNK, chunk * CHUNK)
+            if chunk >= 1:
+                nc.vector.tensor_reduce(
+                    out=sums[:, done],
+                    in_=expd[:, :, done].rearrange("p m t -> p t m"),
+                    axis=AXIS.X,
+                    op=ALU.add,
+                )
+            if chunk < CHUNKS:
+                nc.vector.tensor_reduce(
+                    out=top[:, ts], in_=scores[chunk][:, :, 0:ROWS], axis=AXIS.X, op=ALU.max
+                )
+            if chunk >= 1:
+                nc.vector.reciprocal(out=inverse[:, done], in_=sums[:, done])
+            if chunk < CHUNKS:
+                nc.vector.tensor_tensor(
+                    out=expd[:, :, ts],
+                    in0=scores[chunk][:, :, 0:ROWS].rearrange("p t m -> p m t"),
+                    in1=top[:, ts].unsqueeze(1).to_broadcast([P, ROWS, CHUNK]),
+                    op=ALU.subtract,
+                )
+                nc.scalar.activation(
+                    out=expd[:, :, ts], in_=expd[:, :, ts], func=ACT.Exp, scale=SCALE
+                )
+            if chunk >= 1:
+                nc.vector.tensor_tensor(
+                    out=expd[:, :, done],
+                    in0=expd[:, :, done],
+                    in1=inverse[:, done].unsqueeze(1).to_broadcast([P, ROWS, CHUNK]),
+                    op=ALU.mult,
+                )
+
+        att = keep.tile([P, ROWS * ROWS], F32, align_bytes=64, name="att")
+        nc.vector.transpose(out=att[:], in_=expd[:].rearrange("p m t -> p (m t)"))
+
+        att_view = att[:].rearrange("p (m i) -> p i m", i=ROWS)
+        result = keep.tile([P, HEADS, HEADS], F32, name="result")
+        nc.vector.scalar_tensor_tensor(
+            out=result[:],
+            in0=att_view[:, HEADS:ROWS, HEADS:ROWS],
+            scalar=neg_lam[:, 0:1],
+            in1=att_view[:, 0:HEADS, 0:HEADS],
+            op0=ALU.mult,
+            op1=ALU.add,
+        )
+        nc.sync.dma_start(
+            out=out.rearrange("b n a h -> (b n) (a h)"), in_=result[:].rearrange("p a h -> p (a h)")
+        )

@@ -26,28 +26,23 @@ QUAD = 32
 QUADS = P // QUAD
 BANK = 512
 W_TILES = 4
-PAIRS = 4
-PAIR_HEADS = 8
+TILE_ROWS = 8
+N_TILE = TILE_ROWS * D
 CHUNK = 8
 CHUNKS = QUAD // CHUNK
 SCALE = D ** -0.5
 LAM_INIT = 0.8 - 0.6 * math.exp(-0.3 * 12)
-BURST = 16
+BURST = 8
 SCORE_COLS = 44
 
 FLOPS = 2 * P * K * 2 * K + 2 * P * ROWS * ROWS * D
 
 
-def regroup_rows(nc, banks, ident, row_words, grouped_words):
-    bank = banks.tile([P, 2 * PASSES, P], F32, tag="bank", name="bank")
-    for g in range(PASSES):
+def transpose_words(nc, bank, ident, row_words, g):
+    for e in range(row_words.shape[1]):
         for u in range(2):
             every_2nd = slice(2 * P * g + u, 2 * P * (g + 1), 2)
-            nc.tensor.transpose(bank[:, 2 * g + u, :], row_words[:, every_2nd], ident)
-    nc.scalar.copy(
-        out=grouped_words.rearrange("p (g r u) -> p g r u", g=PASSES, u=2),
-        in_=bank[:].rearrange("p (g u) r -> p g r u", u=2),
-    )
+            nc.tensor.transpose(bank[:, e, u, :], row_words[:, e, every_2nd], ident)
 
 
 def tile_differentialattention_pa_s_kernel(tc, x, Wq, Wk, lq1, lq2, lk1, lk2, out):
@@ -56,19 +51,23 @@ def tile_differentialattention_pa_s_kernel(tc, x, Wq, Wk, lq1, lq2, lk1, lk2, ou
         keep = ctx.enter_context(tc.tile_pool(name="keep", bufs=1))
         stage = ctx.enter_context(tc.tile_pool(name="stage", bufs=4))
         banks = ctx.enter_context(tc.psum_pool(name="banks", bufs=5))
-        y_pool = ctx.enter_context(tc.psum_pool(name="y_pool", bufs=2))
-        idle_pool = ctx.enter_context(tc.psum_pool(name="idle_pool", bufs=1))
+        y_pool = ctx.enter_context(tc.psum_pool(name="y_pool", bufs=3))
         ctx.enter_context(tc.manual_schedule())
 
         x_sb = keep.tile([P, K], BF16, name="x_sb")
-        nc.sync.dma_start(out=x_sb[:], in_=x.rearrange("b n k -> (b n) k"))
         w_tiles = []
         for w in (Wq, Wk):
-            w_view = w.rearrange("(s p j) k -> s p (j k)", p=P, j=2)
-            for s in range(W_TILES):
-                w_sb = keep.tile([P, 2 * K], BF16, name="w_sb%d" % len(w_tiles))
-                nc.sync.dma_start(out=w_sb[:], in_=w_view[s])
-                w_tiles.append(w_sb)
+            w_view = w.rearrange("(s e p j) k -> j s p e k", s=2, e=2, j=2)
+            for j in range(2):
+                for s in range(2):
+                    w_sb = keep.tile([P, 2, K], BF16, name="w_sb%d" % len(w_tiles))
+                    if not w_tiles:
+                        for e in range(2):
+                            nc.sync.dma_start(out=w_sb[:, e], in_=w_view[j, s, :, e])
+                        nc.sync.dma_start(out=x_sb[:], in_=x.rearrange("b n k -> (b n) k"))
+                    else:
+                        nc.sync.dma_start(out=w_sb[:], in_=w_view[j, s])
+                    w_tiles.append(w_sb)
 
         lam_rows = keep.tile([P, 4 * D], BF16, name="lam_rows")
         nc.vector.memset(lam_rows[:], 0.0)
@@ -91,9 +90,9 @@ def tile_differentialattention_pa_s_kernel(tc, x, Wq, Wk, lq1, lq2, lk1, lk2, ou
         nc.vector.quantize_mx(
             out=idle_codes[:].bitcast(FP8X4), scales=idle_scales[:], in_=idle_zeros[:]
         )
-        idle_bank = idle_pool.tile([P, P], F32, name="idle_bank")
 
         def hold_clock(passes):
+            idle_bank = banks.tile([P, P], F32, tag="bank", name="idle_bank")
             for repeat in range(passes):
                 nc.tensor.matmul_mx(
                     out=idle_bank[:],
@@ -106,95 +105,147 @@ def tile_differentialattention_pa_s_kernel(tc, x, Wq, Wk, lq1, lq2, lk1, lk2, ou
                 )
 
         q_blocks = keep.tile([P, QUAD, QUADS, ROWS], F32, name="q_blocks")
-        nc.vector.memset(q_blocks[:], 0.0)
-        k_cols = keep.tile([P, QUAD + 1, ROWS], F32, name="k_cols")
-        nc.vector.memset(k_cols[:, QUAD, :], 0.0)
+        nc.gpsimd.memset(q_blocks[:], 0.0)
+        k_rows = keep.tile([P, SCORE_COLS, QUAD], F32, align_bytes=64, name="k_rows")
+        nc.gpsimd.memset(k_rows[:, ROWS:SCORE_COLS, :], 0.0)
 
-        x_grouped = keep.tile([P, PASSES * P * 4], BF16, align_bytes=64, name="x_grouped")
-        regroup_rows(nc, banks, ident[:], x_sb[:].bitcast(F32), x_grouped[:].bitcast(F32))
-        x_codes = keep.tile([P, PASSES * P], U32, align_bytes=64, name="x_codes")
-        x_scales = keep.tile([P, PASSES * P], U8, align_bytes=64, name="x_scales")
-        nc.vector.quantize_mx(out=x_codes[:].bitcast(FP8X4), scales=x_scales[:], in_=x_grouped[:])
-
+        w_banks = {}
         grouped = {}
         w_codes = {}
         w_scales = {}
 
-        def regroup_tile(n):
-            grouped[n] = stage.tile([P, 2 * PASSES * P * 4], BF16, align_bytes=64, name="grouped")
-            for j in range(2):
-                words = slice(j * WORDS, (j + 1) * WORDS)
-                regroup_rows(
-                    nc,
-                    banks,
-                    ident[:],
-                    w_tiles[n][:].bitcast(F32)[:, words],
-                    grouped[n][:].bitcast(F32)[:, words],
-                )
+        def transpose_tile(n):
+            row_words = w_tiles[n][:].rearrange("p e k -> p (e k)").bitcast(F32)
+            row_words = row_words.rearrange("p (e w) -> p e w", e=2)
+            for g in range(PASSES):
+                w_banks[n, g] = banks.tile([P, 2, 2, P], F32, tag="bank", name="w_bank")
+                transpose_words(nc, w_banks[n, g], ident[:], row_words, g)
 
-        def quantise_tile(n):
-            w_codes[n] = stage.tile([P, 2 * PASSES * P], U32, align_bytes=64, name="w_codes")
-            w_scales[n] = stage.tile([P, 2 * PASSES * P], U8, align_bytes=64, name="w_scales")
+        def empty_banks(n, engines):
+            grouped[n] = stage.tile([P, PASSES, 2, P, 2], F32, align_bytes=64, name="grouped")
+            for g in range(PASSES):
+                source = w_banks[n, g][:].rearrange("p e u r -> p e r u")
+                if engines[g] == "vector":
+                    nc.vector.tensor_copy(out=grouped[n][:, g], in_=source)
+                else:
+                    nc.scalar.copy(out=grouped[n][:, g], in_=source)
+
+        def quantise(n, first, passes):
+            if n not in w_codes:
+                w_codes[n] = stage.tile([P, PASSES * N_TILE], U32, align_bytes=64, name="w_codes")
+                w_scales[n] = stage.tile([P, PASSES * N_TILE], U8, align_bytes=64, name="w_scales")
+            cols = slice(first * N_TILE, (first + passes) * N_TILE)
+            values = grouped[n][:, first : first + passes].rearrange("p g e r u -> p (g e r u)")
             nc.vector.quantize_mx(
-                out=w_codes[n][:].bitcast(FP8X4), scales=w_scales[n][:], in_=grouped[n][:]
+                out=w_codes[n][:, cols].bitcast(FP8X4),
+                scales=w_scales[n][:, cols],
+                in_=values.bitcast(BF16),
             )
 
-        def multiply_tile(n, y_bank):
-            for j in range(2):
-                y_start = j * (BANK // 2) + (n % 2) * P
-                for g in range(PASSES):
-                    x_cols = slice(g * P, (g + 1) * P)
-                    w_cols = slice((j * PASSES + g) * P, (j * PASSES + g + 1) * P)
-                    nc.tensor.matmul_mx(
-                        out=y_bank[:, y_start : y_start + P],
-                        lhsT=x_codes[:, x_cols].bitcast(FP8X4),
-                        lhsT_scale=x_scales[:, x_cols],
-                        rhs=w_codes[n][:, w_cols].bitcast(FP8X4),
-                        rhs_scale=w_scales[n][:, w_cols],
-                        start=(g == 0),
-                        stop=(g == PASSES - 1),
+        def quantise_tile(n):
+            quantise(n, 0, PASSES)
+
+        def quantise_half(n, g):
+            quantise(n, g, 1)
+
+        def multiply_tile(n, y_cols):
+            for g in range(PASSES):
+                x_cols = slice(g * P, (g + 1) * P)
+                w_cols = slice(g * N_TILE, (g + 1) * N_TILE)
+                nc.tensor.matmul_mx(
+                    out=y_cols,
+                    lhsT=x_codes[:, x_cols].bitcast(FP8X4),
+                    lhsT_scale=x_scales[:, x_cols],
+                    rhs=w_codes[n][:, w_cols].bitcast(FP8X4),
+                    rhs_scale=w_scales[n][:, w_cols],
+                    start=(g == 0),
+                    stop=(g == PASSES - 1),
+                )
+
+        def multiply_pair(n):
+            y_bank = y_pool.tile([P, BANK], F32, tag="y_bank", name="y_bank")
+            multiply_tile(n, y_bank[:, 0:N_TILE])
+            multiply_tile(n + 1, y_bank[:, N_TILE : 2 * N_TILE])
+            return y_bank
+
+        def unpack_q(j, y_bank, engines):
+            swapped = stage.tile([P, 2 * TILE_ROWS, QUAD], F32, align_bytes=64, name="swapped")
+            nc.vector.transpose(out=swapped[:].rearrange("p i t -> p (i t)"), in_=y_bank[:])
+            for c in range(QUADS):
+                rows = slice(c * QUAD, (c + 1) * QUAD)
+                target = q_blocks[rows, :, c, j * HEADS : (j + 1) * HEADS]
+                source = swapped[rows].rearrange("p i t -> p t i")
+                if engines[c] == "vector":
+                    nc.vector.tensor_scalar(
+                        out=target, in0=source, scalar1=SCALE, scalar2=None, op0=ALU.mult
+                    )
+                elif engines[c] == "scalar":
+                    nc.scalar.activation(out=target, in_=source, func=ACT.Copy, scale=SCALE)
+                else:
+                    nc.gpsimd.tensor_scalar(
+                        out=target, in0=source, scalar1=SCALE, scalar2=0.0, op0=ALU.mult, op1=ALU.add
                     )
 
-        def unpack_bank(pair, y_bank):
-            swapped = stage.tile([P, BANK], F32, align_bytes=64, name="swapped")
-            nc.vector.transpose(out=swapped[:], in_=y_bank[:])
-            heads = slice((pair % 2) * PAIR_HEADS, (pair % 2 + 1) * PAIR_HEADS)
-            if pair < PAIRS // 2:
-                for c in range(QUADS):
-                    rows = slice(c * QUAD, (c + 1) * QUAD)
-                    source = swapped[rows, :].rearrange("p (j h t) -> p t j h", j=2, t=QUAD)
-                    target = q_blocks[rows, :, c, :].rearrange("p t (j h) -> p t j h", j=2)
-                    if c % 2 == 0:
-                        nc.vector.tensor_copy(out=target[:, :, :, heads], in_=source)
-                    else:
-                        nc.gpsimd.tensor_scalar(
-                            out=target[:, :, :, heads],
-                            in0=source,
-                            scalar1=1.0,
-                            scalar2=0.0,
-                            op0=ALU.mult,
-                            op1=ALU.add,
-                        )
-            else:
-                source = swapped[:].rearrange("p (j h t) -> p t j h", j=2, t=QUAD)
-                target = k_cols[:, 0:QUAD, :].rearrange("p t (j h) -> p t j h", j=2)
-                first = slice(0, QUAD // 2)
-                second = slice(QUAD // 2, QUAD)
-                nc.vector.tensor_copy(out=target[:, first, :, heads], in_=source[:, first])
-                nc.scalar.copy(out=target[:, second, :, heads], in_=source[:, second])
+        def unpack_k(first_row, rows, y_cols):
+            k_flat = k_rows[:, first_row : first_row + rows, :].rearrange("p m t -> p (m t)")
+            nc.vector.transpose(out=k_flat, in_=y_cols)
 
-        for weight in range(2):
-            tiles = range(weight * W_TILES, (weight + 1) * W_TILES)
-            for n in tiles:
-                regroup_tile(n)
-                if n > tiles[0]:
-                    quantise_tile(n - 1)
-            quantise_tile(tiles[-1])
-            for pair in (2 * weight, 2 * weight + 1):
-                y_bank = y_pool.tile([P, BANK], F32, tag="y_bank", name="y_bank")
-                multiply_tile(2 * pair, y_bank)
-                multiply_tile(2 * pair + 1, y_bank)
-                unpack_bank(pair, y_bank)
+        both = ("scalar", "scalar")
+        split = ("scalar", "vector")
+        transpose_tile(0)
+        empty_banks(0, split)
+        x_grouped = keep.tile([P, PASSES, P, 2], F32, align_bytes=64, name="x_grouped")
+        x_bank = banks.tile([P, PASSES, 2, P], F32, tag="bank", name="x_bank")
+        x_words = x_sb[:].bitcast(F32).unsqueeze(1)
+        for g in range(PASSES):
+            transpose_words(nc, x_bank[:, g : g + 1], ident[:], x_words, g)
+        nc.vector.tensor_copy(
+            out=x_grouped[:], in_=x_bank[:].rearrange("p g u r -> p g r u")
+        )
+        x_codes = keep.tile([P, PASSES * P], U32, align_bytes=64, name="x_codes")
+        x_scales = keep.tile([P, PASSES * P], U8, align_bytes=64, name="x_scales")
+        nc.vector.quantize_mx(
+            out=x_codes[:].bitcast(FP8X4),
+            scales=x_scales[:],
+            in_=x_grouped[:].rearrange("p g r u -> p (g r u)").bitcast(BF16),
+        )
+        transpose_tile(1)
+        empty_banks(1, both)
+        quantise_tile(0)
+        transpose_tile(2)
+        empty_banks(2, split)
+        quantise_tile(1)
+        transpose_tile(3)
+        empty_banks(3, both)
+        quantise_tile(2)
+        unpack_q(0, multiply_pair(0), ("gpsimd", "gpsimd", "gpsimd", "gpsimd"))
+        transpose_tile(4)
+        empty_banks(4, both)
+        quantise_tile(3)
+        transpose_tile(5)
+        empty_banks(5, both)
+        quantise_tile(4)
+        y_q1 = multiply_pair(2)
+        transpose_tile(6)
+        empty_banks(6, both)
+        transpose_tile(7)
+        empty_banks(7, both)
+        unpack_q(1, y_q1, ("gpsimd", "gpsimd", "gpsimd", "scalar"))
+        quantise_tile(5)
+        y_k0 = multiply_pair(4)
+        quantise_tile(6)
+        quantise_half(7, 0)
+        quantise_half(7, 1)
+        y_k = {}
+        for n in (6, 7):
+            y_k[n] = y_pool.tile([P, BANK], F32, tag="y_bank", name="y_bank")
+            multiply_tile(n, y_k[n][:, 0:N_TILE])
+        unpack_k(0, HEADS, y_k0[:])
+        for n in (6, 7):
+            for half in range(2):
+                unpack_k(
+                    (n - 4) * TILE_ROWS + half * QUADS, QUADS, y_k[n][:, half * P : (half + 1) * P]
+                )
         hold_clock(BURST)
 
         lam_bank = banks.tile([P, 4 * D], F32, tag="bank", name="lam_bank")
@@ -222,70 +273,88 @@ def tile_differentialattention_pa_s_kernel(tc, x, Wq, Wk, lq1, lq2, lk1, lk2, ou
             op1=ALU.subtract,
         )
 
-        k_flat = k_cols[:].rearrange("p t m -> p (t m)")
         scores = []
         for chunk in range(CHUNKS):
             scores.append(banks.tile([P, CHUNK, SCORE_COLS], F32, tag="bank", name="scores"))
             for t in range(CHUNK):
-                first_col = (chunk * CHUNK + t) * ROWS
                 nc.tensor.matmul(
                     out=scores[chunk][:, t, :],
                     lhsT=q_blocks[:, chunk * CHUNK + t].rearrange("p c i -> p (c i)"),
-                    rhs=k_flat[:, first_col : first_col + SCORE_COLS],
+                    rhs=k_rows[:, :, chunk * CHUNK + t],
                     start=True,
                     stop=True,
                 )
 
-        top = keep.tile([P, QUAD], F32, name="top")
-        expd = keep.tile([P, ROWS, QUAD], F32, align_bytes=64, name="expd")
+        half_weights = keep.tile([P, 2], F32, name="half_weights")
+        ident_halves = ident[:].rearrange("p (c half i) -> p half c i", c=QUADS, half=2)
+        for half in range(2):
+            nc.vector.tensor_reduce(
+                out=half_weights[:, half : half + 1],
+                in_=ident_halves[:, half],
+                axis=AXIS.XY,
+                op=ALU.add,
+            )
+        nc.vector.tensor_tensor(
+            out=half_weights[:, 1:2], in0=half_weights[:, 1:2], in1=neg_lam[:], op=ALU.mult
+        )
+
+        neg_top = keep.tile([P, QUAD], F32, name="neg_top")
+        expd = keep.tile([P, QUAD, ROWS], F32, name="expd")
         sums = keep.tile([P, QUAD], F32, name="sums")
         inverse = keep.tile([P, QUAD], F32, name="inverse")
+        mixed = keep.tile([P, QUAD, HEADS], F32, name="mixed")
+        terms = keep.tile([P, HEADS, QUAD], F32, align_bytes=64, name="terms")
         for chunk in range(CHUNKS + 1):
-            ts = slice(chunk * CHUNK, (chunk + 1) * CHUNK)
-            done = slice((chunk - 1) * CHUNK, chunk * CHUNK)
-            if chunk >= 1:
+            if chunk < CHUNKS:
+                ts = slice(chunk * CHUNK, (chunk + 1) * CHUNK)
                 nc.vector.tensor_reduce(
-                    out=sums[:, done],
-                    in_=expd[:, :, done].rearrange("p m t -> p t m"),
+                    out=neg_top[:, ts],
+                    in_=scores[chunk][:, :, 0:ROWS],
                     axis=AXIS.X,
-                    op=ALU.add,
+                    op=ALU.max,
+                    negate=True,
                 )
-            if chunk < CHUNKS:
-                nc.vector.tensor_reduce(
-                    out=top[:, ts], in_=scores[chunk][:, :, 0:ROWS], axis=AXIS.X, op=ALU.max
-                )
+                for t in range(ts.start, ts.stop):
+                    nc.scalar.activation(
+                        out=expd[:, t, :],
+                        in_=scores[chunk][:, t % CHUNK, 0:ROWS],
+                        func=ACT.Exp,
+                        bias=neg_top[:, t : t + 1],
+                        accum_out=sums[:, t : t + 1],
+                    )
             if chunk >= 1:
+                done = slice((chunk - 1) * CHUNK, chunk * CHUNK)
+                nc.vector.tensor_scalar(
+                    out=mixed[:, done],
+                    in0=expd[:, done, 0:HEADS],
+                    scalar1=half_weights[:, 0:1],
+                    scalar2=None,
+                    op0=ALU.mult,
+                )
                 nc.vector.reciprocal(out=inverse[:, done], in_=sums[:, done])
-            if chunk < CHUNKS:
-                nc.vector.tensor_tensor(
-                    out=expd[:, :, ts],
-                    in0=scores[chunk][:, :, 0:ROWS].rearrange("p t m -> p m t"),
-                    in1=top[:, ts].unsqueeze(1).to_broadcast([P, ROWS, CHUNK]),
-                    op=ALU.subtract,
+                nc.vector.scalar_tensor_tensor(
+                    out=mixed[:, done],
+                    in0=expd[:, done, HEADS:ROWS],
+                    scalar=half_weights[:, 1:2],
+                    in1=mixed[:, done],
+                    op0=ALU.mult,
+                    op1=ALU.add,
                 )
-                nc.scalar.activation(
-                    out=expd[:, :, ts], in_=expd[:, :, ts], func=ACT.Exp, scale=SCALE
-                )
-            if chunk >= 1:
                 nc.vector.tensor_tensor(
-                    out=expd[:, :, done],
-                    in0=expd[:, :, done],
-                    in1=inverse[:, done].unsqueeze(1).to_broadcast([P, ROWS, CHUNK]),
+                    out=terms[:, :, done],
+                    in0=mixed[:, done].rearrange("p t h -> p h t"),
+                    in1=inverse[:, done].unsqueeze(1).to_broadcast([P, HEADS, CHUNK]),
                     op=ALU.mult,
                 )
 
-        att = keep.tile([P, ROWS * ROWS], F32, align_bytes=64, name="att")
-        nc.vector.transpose(out=att[:], in_=expd[:].rearrange("p m t -> p (m t)"))
-
-        att_view = att[:].rearrange("p (m i) -> p i m", i=ROWS)
+        rows_t = keep.tile([P, HEADS, ROWS], F32, align_bytes=64, name="rows_t")
+        nc.vector.transpose(
+            out=rows_t[:].rearrange("p h i -> p (h i)"), in_=terms[:].rearrange("p h t -> p (h t)")
+        )
+        by_row = rows_t[:].rearrange("p h i -> p i h")
         result = keep.tile([P, HEADS, HEADS], F32, name="result")
-        nc.vector.scalar_tensor_tensor(
-            out=result[:],
-            in0=att_view[:, HEADS:ROWS, HEADS:ROWS],
-            scalar=neg_lam[:, 0:1],
-            in1=att_view[:, 0:HEADS, 0:HEADS],
-            op0=ALU.mult,
-            op1=ALU.add,
+        nc.vector.tensor_tensor(
+            out=result[:], in0=by_row[:, 0:HEADS], in1=by_row[:, HEADS:ROWS], op=ALU.add
         )
         nc.sync.dma_start(
             out=out.rearrange("b n a h -> (b n) (a h)"), in_=result[:].rearrange("p a h -> p (a h)")

@@ -28,12 +28,11 @@ BANK = 512
 W_TILES = 4
 TILE_ROWS = 8
 N_TILE = TILE_ROWS * D
-CHUNK = 8
-CHUNKS = QUAD // CHUNK
+CHUNK_SIZES = (8, 8, 8, 4, 4)
 SCALE = D ** -0.5
 LAM_INIT = 0.8 - 0.6 * math.exp(-0.3 * 12)
 BURST = 8
-SCORE_COLS = 44
+SCORE_COLS = 48
 
 FLOPS = 2 * P * K * 2 * K + 2 * P * ROWS * ROWS * D
 
@@ -78,34 +77,15 @@ def tile_differentialattention_pa_s_kernel(tc, x, Wq, Wk, lq1, lq2, lk1, lk2, ou
 
         ident = keep.tile([P, P], F32, name="ident")
         make_identity(nc, ident[:])
-        ones = keep.tile([P, P], BF16, name="ones")
+        ones = keep.tile([P, P], F32, name="ones")
         nc.vector.memset(ones[:], 1.0)
         warm = keep.tile([P, 2], F32, name="warm")
         nc.vector.memset(warm[:], 0.0)
         nc.scalar.activation(out=warm[:, 1:2], in_=warm[:, 0:1], func=ACT.Exp)
-        idle_zeros = keep.tile([P, 4 * P], BF16, align_bytes=64, name="idle_zeros")
-        idle_codes = keep.tile([P, P], U32, align_bytes=64, name="idle_codes")
-        idle_scales = keep.tile([P, P], U8, align_bytes=64, name="idle_scales")
-        nc.vector.memset(idle_zeros[:].bitcast(I32), 0)
-        nc.vector.quantize_mx(
-            out=idle_codes[:].bitcast(FP8X4), scales=idle_scales[:], in_=idle_zeros[:]
-        )
-
-        def hold_clock(passes):
-            idle_bank = banks.tile([P, P], F32, tag="bank", name="idle_bank")
-            for repeat in range(passes):
-                nc.tensor.matmul_mx(
-                    out=idle_bank[:],
-                    lhsT=idle_codes[:].bitcast(FP8X4),
-                    lhsT_scale=idle_scales[:],
-                    rhs=idle_codes[:].bitcast(FP8X4),
-                    rhs_scale=idle_scales[:],
-                    start=True,
-                    stop=True,
-                )
-
         q_blocks = keep.tile([P, QUAD, QUADS, ROWS], F32, name="q_blocks")
-        nc.gpsimd.memset(q_blocks[:], 0.0)
+        nc.vector.memset(q_blocks[:, 0 : QUAD // 2], 0.0)
+        nc.gpsimd.memset(q_blocks[:, QUAD // 2 : QUAD], 0.0)
+        q_rows = keep.tile([P, ROWS, QUAD], F32, align_bytes=64, name="q_rows")
         k_rows = keep.tile([P, SCORE_COLS, QUAD], F32, align_bytes=64, name="k_rows")
         nc.gpsimd.memset(k_rows[:, ROWS:SCORE_COLS, :], 0.0)
 
@@ -168,27 +148,22 @@ def tile_differentialattention_pa_s_kernel(tc, x, Wq, Wk, lq1, lq2, lk1, lk2, ou
             multiply_tile(n + 1, y_bank[:, N_TILE : 2 * N_TILE])
             return y_bank
 
-        def unpack_q(j, y_bank, engines):
-            swapped = stage.tile([P, 2 * TILE_ROWS, QUAD], F32, align_bytes=64, name="swapped")
-            nc.vector.transpose(out=swapped[:].rearrange("p i t -> p (i t)"), in_=y_bank[:])
+        def unpack(rows_tile, first_row, rows, y_cols):
+            target = rows_tile[:, first_row : first_row + rows, :].rearrange("p i t -> p (i t)")
+            nc.vector.transpose(out=target, in_=y_cols)
+
+        def fill_blocks(first_t, tokens, engine):
+            ts = slice(first_t, first_t + tokens)
             for c in range(QUADS):
                 rows = slice(c * QUAD, (c + 1) * QUAD)
-                target = q_blocks[rows, :, c, j * HEADS : (j + 1) * HEADS]
-                source = swapped[rows].rearrange("p i t -> p t i")
-                if engines[c] == "vector":
+                target = q_blocks[rows, ts, c, :].rearrange("p t (b i) -> p b t i", i=4)
+                source = q_rows[rows, :, ts].rearrange("p (b i) t -> p b t i", i=4)
+                if engine == "vector":
                     nc.vector.tensor_scalar(
                         out=target, in0=source, scalar1=SCALE, scalar2=None, op0=ALU.mult
                     )
-                elif engines[c] == "scalar":
-                    nc.scalar.activation(out=target, in_=source, func=ACT.Copy, scale=SCALE)
                 else:
-                    nc.gpsimd.tensor_scalar(
-                        out=target, in0=source, scalar1=SCALE, scalar2=0.0, op0=ALU.mult, op1=ALU.add
-                    )
-
-        def unpack_k(first_row, rows, y_cols):
-            k_flat = k_rows[:, first_row : first_row + rows, :].rearrange("p m t -> p (m t)")
-            nc.vector.transpose(out=k_flat, in_=y_cols)
+                    nc.scalar.activation(out=target, in_=source, func=ACT.Copy, scale=SCALE)
 
         both = ("scalar", "scalar")
         split = ("scalar", "vector")
@@ -215,10 +190,19 @@ def tile_differentialattention_pa_s_kernel(tc, x, Wq, Wk, lq1, lq2, lk1, lk2, ou
         transpose_tile(2)
         empty_banks(2, split)
         quantise_tile(1)
+        lam_prod = keep.tile([P, 2, D], F32, name="lam_prod")
+        nc.vector.tensor_tensor(
+            out=lam_prod[:].rearrange("p n d -> p (n d)"),
+            in0=lam_rows[:, 0 : 2 * D],
+            in1=lam_rows[:, 2 * D : 4 * D],
+            op=ALU.mult,
+        )
+        lam_dots = keep.tile([P, 2], F32, name="lam_dots")
+        nc.vector.tensor_reduce(out=lam_dots[:], in_=lam_prod[:], axis=AXIS.X, op=ALU.add)
         transpose_tile(3)
         empty_banks(3, both)
         quantise_tile(2)
-        unpack_q(0, multiply_pair(0), ("gpsimd", "gpsimd", "gpsimd", "gpsimd"))
+        unpack(q_rows, 0, HEADS, multiply_pair(0)[:])
         transpose_tile(4)
         empty_banks(4, both)
         quantise_tile(3)
@@ -230,73 +214,42 @@ def tile_differentialattention_pa_s_kernel(tc, x, Wq, Wk, lq1, lq2, lk1, lk2, ou
         empty_banks(6, both)
         transpose_tile(7)
         empty_banks(7, both)
-        unpack_q(1, y_q1, ("gpsimd", "gpsimd", "gpsimd", "scalar"))
+        unpack(q_rows, HEADS, HEADS, y_q1[:])
         quantise_tile(5)
+        fill_blocks(0, 4, "vector")
         y_k0 = multiply_pair(4)
         quantise_tile(6)
         quantise_half(7, 0)
         quantise_half(7, 1)
+        fill_blocks(4, 4, "scalar")
         y_k = {}
         for n in (6, 7):
             y_k[n] = y_pool.tile([P, BANK], F32, tag="y_bank", name="y_bank")
             multiply_tile(n, y_k[n][:, 0:N_TILE])
-        unpack_k(0, HEADS, y_k0[:])
+        unpack(k_rows, 0, HEADS, y_k0[:])
         for n in (6, 7):
             for half in range(2):
-                unpack_k(
-                    (n - 4) * TILE_ROWS + half * QUADS, QUADS, y_k[n][:, half * P : (half + 1) * P]
+                unpack(
+                    k_rows,
+                    (n - 4) * TILE_ROWS + half * QUADS,
+                    QUADS,
+                    y_k[n][:, half * P : (half + 1) * P],
                 )
-        hold_clock(BURST)
+        fill_blocks(8, 8, "scalar")
+        fill_blocks(16, 8, "vector")
+        fill_blocks(24, 8, "scalar")
 
-        lam_bank = banks.tile([P, 4 * D], F32, tag="bank", name="lam_bank")
-        nc.tensor.matmul(out=lam_bank[:], lhsT=ones[:], rhs=lam_rows[:], start=True, stop=True)
-        lam_all = keep.tile([P, 4 * D], F32, name="lam_all")
-        nc.scalar.copy(out=lam_all[:], in_=lam_bank[:])
-        lam_prod = keep.tile([P, 2, D], F32, name="lam_prod")
-        nc.vector.tensor_tensor(
-            out=lam_prod[:].rearrange("p n d -> p (n d)"),
-            in0=lam_all[:, 0 : 2 * D],
-            in1=lam_all[:, 2 * D : 4 * D],
-            op=ALU.mult,
-        )
-        lam_dots = keep.tile([P, 2], F32, name="lam_dots")
-        nc.vector.tensor_reduce(out=lam_dots[:], in_=lam_prod[:], axis=AXIS.X, op=ALU.add)
-        lam_exp = keep.tile([P, 2], F32, name="lam_exp")
-        nc.scalar.activation(out=lam_exp[:], in_=lam_dots[:], func=ACT.Exp)
-        neg_lam = keep.tile([P, 1], F32, name="neg_lam")
-        nc.vector.scalar_tensor_tensor(
-            out=neg_lam[:],
-            in0=lam_exp[:, 1:2],
-            scalar=-LAM_INIT,
-            in1=lam_exp[:, 0:1],
-            op0=ALU.add,
-            op1=ALU.subtract,
-        )
-
-        scores = []
-        for chunk in range(CHUNKS):
-            scores.append(banks.tile([P, CHUNK, SCORE_COLS], F32, tag="bank", name="scores"))
-            for t in range(CHUNK):
-                nc.tensor.matmul(
-                    out=scores[chunk][:, t, :],
-                    lhsT=q_blocks[:, chunk * CHUNK + t].rearrange("p c i -> p (c i)"),
-                    rhs=k_rows[:, :, chunk * CHUNK + t],
-                    start=True,
-                    stop=True,
-                )
-
-        half_weights = keep.tile([P, 2], F32, name="half_weights")
-        ident_halves = ident[:].rearrange("p (c half i) -> p half c i", c=QUADS, half=2)
-        for half in range(2):
-            nc.vector.tensor_reduce(
-                out=half_weights[:, half : half + 1],
-                in_=ident_halves[:, half],
-                axis=AXIS.XY,
-                op=ALU.add,
+        idle_bank = banks.tile([P, N_TILE], F32, tag="bank", name="idle_bank")
+        for repeat in range(BURST):
+            nc.tensor.matmul_mx(
+                out=idle_bank[:],
+                lhsT=x_codes[:, 0:P].bitcast(FP8X4),
+                lhsT_scale=x_scales[:, 0:P],
+                rhs=w_codes[7][:, 0:N_TILE].bitcast(FP8X4),
+                rhs_scale=w_scales[7][:, 0:N_TILE],
+                start=True,
+                stop=True,
             )
-        nc.vector.tensor_tensor(
-            out=half_weights[:, 1:2], in0=half_weights[:, 1:2], in1=neg_lam[:], op=ALU.mult
-        )
 
         neg_top = keep.tile([P, QUAD], F32, name="neg_top")
         expd = keep.tile([P, QUAD, ROWS], F32, name="expd")
@@ -304,57 +257,107 @@ def tile_differentialattention_pa_s_kernel(tc, x, Wq, Wk, lq1, lq2, lk1, lk2, ou
         inverse = keep.tile([P, QUAD], F32, name="inverse")
         mixed = keep.tile([P, QUAD, HEADS], F32, name="mixed")
         terms = keep.tile([P, HEADS, QUAD], F32, align_bytes=64, name="terms")
-        for chunk in range(CHUNKS + 1):
-            if chunk < CHUNKS:
-                ts = slice(chunk * CHUNK, (chunk + 1) * CHUNK)
-                nc.vector.tensor_reduce(
-                    out=neg_top[:, ts],
-                    in_=scores[chunk][:, :, 0:ROWS],
-                    axis=AXIS.X,
-                    op=ALU.max,
-                    negate=True,
+        half_weights = keep.tile([P, 2], F32, name="half_weights")
+
+        def score(ts):
+            bank = banks.tile([P, ts.stop - ts.start, SCORE_COLS], F32, tag="bank", name="scores")
+            for t in range(ts.start, ts.stop):
+                nc.tensor.matmul(
+                    out=bank[:, t - ts.start, :],
+                    lhsT=q_blocks[:, t].rearrange("p c i -> p (c i)"),
+                    rhs=k_rows[:, :, t],
+                    start=True,
+                    stop=True,
                 )
-                for t in range(ts.start, ts.stop):
-                    nc.scalar.activation(
-                        out=expd[:, t, :],
-                        in_=scores[chunk][:, t % CHUNK, 0:ROWS],
-                        func=ACT.Exp,
-                        bias=neg_top[:, t : t + 1],
-                        accum_out=sums[:, t : t + 1],
+            return bank
+
+        def exponentiate(ts, bank):
+            nc.vector.tensor_reduce(
+                out=neg_top[:, ts], in_=bank[:, :, 0:ROWS], axis=AXIS.X, op=ALU.max, negate=True
+            )
+            for t in range(ts.start, ts.stop):
+                nc.scalar.activation(
+                    out=expd[:, t, :],
+                    in_=bank[:, t - ts.start, 0:ROWS],
+                    func=ACT.Exp,
+                    bias=neg_top[:, t : t + 1],
+                    accum_out=sums[:, t : t + 1],
+                )
+
+        def normalise(ts):
+            nc.vector.tensor_scalar(
+                out=mixed[:, ts],
+                in0=expd[:, ts, 0:HEADS],
+                scalar1=half_weights[:, 0:1],
+                scalar2=None,
+                op0=ALU.mult,
+            )
+            nc.vector.reciprocal(out=inverse[:, ts], in_=sums[:, ts])
+            nc.vector.scalar_tensor_tensor(
+                out=mixed[:, ts],
+                in0=expd[:, ts, HEADS:ROWS],
+                scalar=half_weights[:, 1:2],
+                in1=mixed[:, ts],
+                op0=ALU.mult,
+                op1=ALU.add,
+            )
+            blocks = (ts.stop - ts.start) // 4
+            factor = inverse[:, ts].rearrange("p (b t) -> p b t", t=4)
+            nc.vector.tensor_tensor(
+                out=terms[:, :, ts].rearrange("p h (b t) -> p b h t", t=4),
+                in0=mixed[:, ts].rearrange("p (b t) h -> p b h t", t=4),
+                in1=factor.unsqueeze(2).to_broadcast([P, blocks, HEADS, 4]),
+                op=ALU.mult,
+            )
+
+        before = None
+        for size in CHUNK_SIZES:
+            first_t = 0 if before is None else before.stop
+            ts = slice(first_t, first_t + size)
+            exponentiate(ts, score(ts))
+            if before is None:
+                lam_bank = banks.tile([P, 2], F32, tag="bank", name="lam_bank")
+                nc.tensor.matmul(
+                    out=lam_bank[:], lhsT=ones[:], rhs=lam_dots[:], start=True, stop=True
+                )
+                lam_exp = keep.tile([P, 2], F32, name="lam_exp")
+                nc.scalar.activation(out=lam_exp[:], in_=lam_bank[:], func=ACT.Exp)
+                ident_halves = ident[:].rearrange("p (c half i) -> p half c i", c=QUADS, half=2)
+                for half in range(2):
+                    nc.vector.tensor_reduce(
+                        out=half_weights[:, half : half + 1],
+                        in_=ident_halves[:, half],
+                        axis=AXIS.XY,
+                        op=ALU.add,
                     )
-            if chunk >= 1:
-                done = slice((chunk - 1) * CHUNK, chunk * CHUNK)
-                nc.vector.tensor_scalar(
-                    out=mixed[:, done],
-                    in0=expd[:, done, 0:HEADS],
-                    scalar1=half_weights[:, 0:1],
-                    scalar2=None,
-                    op0=ALU.mult,
-                )
-                nc.vector.reciprocal(out=inverse[:, done], in_=sums[:, done])
+                neg_lam = keep.tile([P, 1], F32, name="neg_lam")
                 nc.vector.scalar_tensor_tensor(
-                    out=mixed[:, done],
-                    in0=expd[:, done, HEADS:ROWS],
-                    scalar=half_weights[:, 1:2],
-                    in1=mixed[:, done],
-                    op0=ALU.mult,
-                    op1=ALU.add,
+                    out=neg_lam[:],
+                    in0=lam_exp[:, 1:2],
+                    scalar=-LAM_INIT,
+                    in1=lam_exp[:, 0:1],
+                    op0=ALU.add,
+                    op1=ALU.subtract,
                 )
                 nc.vector.tensor_tensor(
-                    out=terms[:, :, done],
-                    in0=mixed[:, done].rearrange("p t h -> p h t"),
-                    in1=inverse[:, done].unsqueeze(1).to_broadcast([P, HEADS, CHUNK]),
-                    op=ALU.mult,
+                    out=half_weights[:, 1:2], in0=half_weights[:, 1:2], in1=neg_lam[:], op=ALU.mult
                 )
+            else:
+                normalise(before)
+            before = ts
+        normalise(before)
 
         rows_t = keep.tile([P, HEADS, ROWS], F32, align_bytes=64, name="rows_t")
         nc.vector.transpose(
             out=rows_t[:].rearrange("p h i -> p (h i)"), in_=terms[:].rearrange("p h t -> p (h t)")
         )
-        by_row = rows_t[:].rearrange("p h i -> p i h")
         result = keep.tile([P, HEADS, HEADS], F32, name="result")
+        by_rows = rows_t[:].rearrange("p h (half b a) -> p half b h a", half=2, a=4)
         nc.vector.tensor_tensor(
-            out=result[:], in0=by_row[:, 0:HEADS], in1=by_row[:, HEADS:ROWS], op=ALU.add
+            out=result[:].rearrange("p (b a) h -> p b h a", a=4),
+            in0=by_rows[:, 0],
+            in1=by_rows[:, 1],
+            op=ALU.add,
         )
         nc.sync.dma_start(
             out=out.rearrange("b n a h -> (b n) (a h)"), in_=result[:].rearrange("p a h -> p (a h)")

@@ -31,7 +31,7 @@ N_TILE = TILE_ROWS * D
 CHUNK_SIZES = (8, 8, 8, 4, 4)
 SCALE = D ** -0.5
 LAM_INIT = 0.8 - 0.6 * math.exp(-0.3 * 12)
-BURST = 8
+BURST = 6
 SCORE_COLS = 48
 
 FLOPS = 2 * P * K * 2 * K + 2 * P * ROWS * ROWS * D
@@ -200,22 +200,23 @@ def tile_differentialattention_pa_s_kernel(tc, x, Wq, Wk, lq1, lq2, lk1, lk2, ou
         lam_dots = keep.tile([P, 2], F32, name="lam_dots")
         nc.vector.tensor_reduce(out=lam_dots[:], in_=lam_prod[:], axis=AXIS.X, op=ALU.add)
         transpose_tile(3)
-        empty_banks(3, both)
+        empty_banks(3, split)
         quantise_tile(2)
-        unpack(q_rows, 0, HEADS, multiply_pair(0)[:])
         transpose_tile(4)
         empty_banks(4, both)
         quantise_tile(3)
         transpose_tile(5)
         empty_banks(5, both)
         quantise_tile(4)
+        y_q0 = multiply_pair(0)
         y_q1 = multiply_pair(2)
+        unpack(q_rows, 0, HEADS, y_q0[:])
         transpose_tile(6)
         empty_banks(6, both)
         transpose_tile(7)
         empty_banks(7, both)
-        unpack(q_rows, HEADS, HEADS, y_q1[:])
         quantise_tile(5)
+        unpack(q_rows, HEADS, HEADS, y_q1[:])
         fill_blocks(0, 4, "vector")
         y_k0 = multiply_pair(4)
         quantise_tile(6)
@@ -237,6 +238,12 @@ def tile_differentialattention_pa_s_kernel(tc, x, Wq, Wk, lq1, lq2, lk1, lk2, ou
                 )
         fill_blocks(8, 8, "scalar")
         fill_blocks(16, 8, "vector")
+
+        lam_bank = banks.tile([P, 2], F32, tag="bank", name="lam_bank")
+        nc.tensor.matmul(out=lam_bank[:], lhsT=ones[:], rhs=lam_dots[:], start=True, stop=True)
+        lam_exp = keep.tile([P, 2], F32, name="lam_exp")
+        nc.scalar.activation(out=lam_exp[:], in_=lam_bank[:], func=ACT.Exp)
+
         fill_blocks(24, 8, "scalar")
 
         idle_bank = banks.tile([P, N_TILE], F32, tag="bank", name="idle_bank")
@@ -258,6 +265,15 @@ def tile_differentialattention_pa_s_kernel(tc, x, Wq, Wk, lq1, lq2, lk1, lk2, ou
         mixed = keep.tile([P, QUAD, HEADS], F32, name="mixed")
         terms = keep.tile([P, HEADS, QUAD], F32, align_bytes=64, name="terms")
         half_weights = keep.tile([P, 2], F32, name="half_weights")
+
+        ident_halves = ident[:].rearrange("p (c half i) -> p half c i", c=QUADS, half=2)
+        for half in range(2):
+            nc.vector.tensor_reduce(
+                out=half_weights[:, half : half + 1],
+                in_=ident_halves[:, half],
+                axis=AXIS.XY,
+                op=ALU.add,
+            )
 
         def score(ts):
             bank = banks.tile([P, ts.stop - ts.start, SCORE_COLS], F32, tag="bank", name="scores")
@@ -316,20 +332,6 @@ def tile_differentialattention_pa_s_kernel(tc, x, Wq, Wk, lq1, lq2, lk1, lk2, ou
             ts = slice(first_t, first_t + size)
             exponentiate(ts, score(ts))
             if before is None:
-                lam_bank = banks.tile([P, 2], F32, tag="bank", name="lam_bank")
-                nc.tensor.matmul(
-                    out=lam_bank[:], lhsT=ones[:], rhs=lam_dots[:], start=True, stop=True
-                )
-                lam_exp = keep.tile([P, 2], F32, name="lam_exp")
-                nc.scalar.activation(out=lam_exp[:], in_=lam_bank[:], func=ACT.Exp)
-                ident_halves = ident[:].rearrange("p (c half i) -> p half c i", c=QUADS, half=2)
-                for half in range(2):
-                    nc.vector.tensor_reduce(
-                        out=half_weights[:, half : half + 1],
-                        in_=ident_halves[:, half],
-                        axis=AXIS.XY,
-                        op=ALU.add,
-                    )
                 neg_lam = keep.tile([P, 1], F32, name="neg_lam")
                 nc.vector.scalar_tensor_tensor(
                     out=neg_lam[:],

@@ -40,8 +40,7 @@ FLOPS = 2 * P * K * 2 * K + 2 * P * ROWS * ROWS * D
 def transpose_words(nc, bank, ident, row_words, g):
     for e in range(row_words.shape[1]):
         for u in range(2):
-            every_2nd = slice(2 * P * g + u, 2 * P * (g + 1), 2)
-            nc.tensor.transpose(bank[:, e, u, :], row_words[:, e, every_2nd], ident)
+            nc.tensor.transpose(bank[:, e, u, :], row_words[:, e, g, u, :], ident)
 
 
 def tile_differentialattention_pa_s_kernel(tc, x, Wq, Wk, lq1, lq2, lk1, lk2, out):
@@ -94,9 +93,21 @@ def tile_differentialattention_pa_s_kernel(tc, x, Wq, Wk, lq1, lq2, lk1, lk2, ou
         w_codes = {}
         w_scales = {}
 
+        sorted_words = {}
+
+        def words_of_tile(n):
+            words = w_tiles[n][:].rearrange("r e k -> r (e k)").bitcast(F32)
+            return words.rearrange("r (e g p u) -> r e g u p", e=2, g=PASSES, u=2)
+
+        def sort_words(n):
+            sorted_words[n] = stage.tile([P, 2, PASSES, 2, P], F32, name="sorted_words")
+            nc.vector.tensor_copy(
+                out=sorted_words[n][:].rearrange("r e g u p -> r (e g) u p"),
+                in_=words_of_tile(n).rearrange("r e g u p -> r (e g) u p"),
+            )
+
         def transpose_tile(n):
-            row_words = w_tiles[n][:].rearrange("p e k -> p (e k)").bitcast(F32)
-            row_words = row_words.rearrange("p (e w) -> p e w", e=2)
+            row_words = sorted_words[n][:] if n in sorted_words else words_of_tile(n)
             for g in range(PASSES):
                 w_banks[n, g] = banks.tile([P, 2, 2, P], F32, tag="bank", name="w_bank")
                 transpose_words(nc, w_banks[n, g], ident[:], row_words, g)
@@ -171,7 +182,7 @@ def tile_differentialattention_pa_s_kernel(tc, x, Wq, Wk, lq1, lq2, lk1, lk2, ou
         empty_banks(0, split)
         x_grouped = keep.tile([P, PASSES, P, 2], F32, align_bytes=64, name="x_grouped")
         x_bank = banks.tile([P, PASSES, 2, P], F32, tag="bank", name="x_bank")
-        x_words = x_sb[:].bitcast(F32).unsqueeze(1)
+        x_words = x_sb[:].bitcast(F32).rearrange("r (e g p u) -> r e g u p", e=1, g=PASSES, u=2)
         for g in range(PASSES):
             transpose_words(nc, x_bank[:, g : g + 1], ident[:], x_words, g)
         nc.vector.tensor_copy(
@@ -187,9 +198,6 @@ def tile_differentialattention_pa_s_kernel(tc, x, Wq, Wk, lq1, lq2, lk1, lk2, ou
         transpose_tile(1)
         empty_banks(1, both)
         quantise_tile(0)
-        transpose_tile(2)
-        empty_banks(2, split)
-        quantise_tile(1)
         lam_prod = keep.tile([P, 2, D], F32, name="lam_prod")
         nc.vector.tensor_tensor(
             out=lam_prod[:].rearrange("p n d -> p (n d)"),
@@ -199,25 +207,32 @@ def tile_differentialattention_pa_s_kernel(tc, x, Wq, Wk, lq1, lq2, lk1, lk2, ou
         )
         lam_dots = keep.tile([P, 2], F32, name="lam_dots")
         nc.vector.tensor_reduce(out=lam_dots[:], in_=lam_prod[:], axis=AXIS.X, op=ALU.add)
+        transpose_tile(2)
+        empty_banks(2, both)
+        quantise_tile(1)
         transpose_tile(3)
-        empty_banks(3, split)
+        empty_banks(3, both)
+        y_q0 = multiply_pair(0)
+        sort_words(4)
         quantise_tile(2)
         transpose_tile(4)
         empty_banks(4, both)
-        quantise_tile(3)
+        sort_words(5)
+        unpack(q_rows, 0, HEADS, y_q0[:])
         transpose_tile(5)
         empty_banks(5, both)
-        quantise_tile(4)
-        y_q0 = multiply_pair(0)
+        quantise_tile(3)
+        sort_words(6)
         y_q1 = multiply_pair(2)
-        unpack(q_rows, 0, HEADS, y_q0[:])
         transpose_tile(6)
         empty_banks(6, both)
+        sort_words(7)
+        quantise_tile(4)
+        unpack(q_rows, HEADS, HEADS, y_q1[:])
         transpose_tile(7)
         empty_banks(7, both)
         quantise_tile(5)
-        unpack(q_rows, HEADS, HEADS, y_q1[:])
-        fill_blocks(0, 4, "vector")
+        fill_blocks(0, 4, "scalar")
         y_k0 = multiply_pair(4)
         quantise_tile(6)
         quantise_half(7, 0)

@@ -24,6 +24,7 @@ ROWS = 2 * HEADS
 D = 32
 QUAD = 32
 QUADS = P // QUAD
+BOTH_PASSES = tuple(range(PASSES))
 BANK = 512
 W_TILES = 4
 TILE_ROWS = 8
@@ -31,8 +32,9 @@ N_TILE = TILE_ROWS * D
 CHUNK_SIZES = (8, 8, 8, 4, 4)
 SCALE = D ** -0.5
 LAM_INIT = 0.8 - 0.6 * math.exp(-0.3 * 12)
-BURST = 6
-SCORE_COLS = 48
+H_HALVES = (slice(0, HEADS // 2), slice(HEADS // 2, HEADS))
+BURST = 7
+SCORE_COLS = (64, 44, 44, 44, 44)
 
 FLOPS = 2 * P * K * 2 * K + 2 * P * ROWS * ROWS * D
 
@@ -48,6 +50,7 @@ def tile_differentialattention_pa_s_kernel(tc, x, Wq, Wk, lq1, lq2, lk1, lk2, ou
     with ExitStack() as ctx:
         keep = ctx.enter_context(tc.tile_pool(name="keep", bufs=1))
         stage = ctx.enter_context(tc.tile_pool(name="stage", bufs=4))
+        row_codes = ctx.enter_context(tc.tile_pool(name="row_codes", bufs=3))
         banks = ctx.enter_context(tc.psum_pool(name="banks", bufs=5))
         y_pool = ctx.enter_context(tc.psum_pool(name="y_pool", bufs=3))
         ctx.enter_context(tc.manual_schedule())
@@ -85,8 +88,8 @@ def tile_differentialattention_pa_s_kernel(tc, x, Wq, Wk, lq1, lq2, lk1, lk2, ou
         nc.vector.memset(q_blocks[:, 0 : QUAD // 2], 0.0)
         nc.gpsimd.memset(q_blocks[:, QUAD // 2 : QUAD], 0.0)
         q_rows = keep.tile([P, ROWS, QUAD], F32, align_bytes=64, name="q_rows")
-        k_rows = keep.tile([P, SCORE_COLS, QUAD], F32, align_bytes=64, name="k_rows")
-        nc.gpsimd.memset(k_rows[:, ROWS:SCORE_COLS, :], 0.0)
+        k_rows = keep.tile([P, max(SCORE_COLS), QUAD], F32, align_bytes=64, name="k_rows")
+        nc.gpsimd.memset(k_rows[:, ROWS:, :], 0.0)
 
         w_banks = {}
         grouped = {}
@@ -121,37 +124,32 @@ def tile_differentialattention_pa_s_kernel(tc, x, Wq, Wk, lq1, lq2, lk1, lk2, ou
                 else:
                     nc.scalar.copy(out=grouped[n][:, g], in_=source)
 
-        def quantise(n, first, passes):
-            if n not in w_codes:
-                w_codes[n] = stage.tile([P, PASSES * N_TILE], U32, align_bytes=64, name="w_codes")
-                w_scales[n] = stage.tile([P, PASSES * N_TILE], U8, align_bytes=64, name="w_scales")
-            cols = slice(first * N_TILE, (first + passes) * N_TILE)
-            values = grouped[n][:, first : first + passes].rearrange("p g e r u -> p (g e r u)")
+        def quantise_tile(n):
+            w_codes[n] = stage.tile([P, PASSES * N_TILE], U32, align_bytes=64, name="w_codes")
+            w_scales[n] = stage.tile([P, PASSES * N_TILE], U8, align_bytes=64, name="w_scales")
             nc.vector.quantize_mx(
-                out=w_codes[n][:, cols].bitcast(FP8X4),
-                scales=w_scales[n][:, cols],
-                in_=values.bitcast(BF16),
+                out=w_codes[n][:].bitcast(FP8X4),
+                scales=w_scales[n][:],
+                in_=grouped[n][:].rearrange("p g e r u -> p (g e r u)").bitcast(BF16),
             )
 
-        def quantise_tile(n):
-            quantise(n, 0, PASSES)
-
-        def quantise_half(n, g):
-            quantise(n, g, 1)
-
-        def multiply_tile(n, y_cols):
+        def multiply(codes, scales, y_cols):
+            width = y_cols.shape[1]
             for g in range(PASSES):
                 x_cols = slice(g * P, (g + 1) * P)
-                w_cols = slice(g * N_TILE, (g + 1) * N_TILE)
+                w_cols = slice(g * width, (g + 1) * width)
                 nc.tensor.matmul_mx(
                     out=y_cols,
                     lhsT=x_codes[:, x_cols].bitcast(FP8X4),
                     lhsT_scale=x_scales[:, x_cols],
-                    rhs=w_codes[n][:, w_cols].bitcast(FP8X4),
-                    rhs_scale=w_scales[n][:, w_cols],
+                    rhs=codes[:, w_cols].bitcast(FP8X4),
+                    rhs_scale=scales[:, w_cols],
                     start=(g == 0),
                     stop=(g == PASSES - 1),
                 )
+
+        def multiply_tile(n, y_cols):
+            multiply(w_codes[n], w_scales[n], y_cols)
 
         def multiply_pair(n):
             y_bank = y_pool.tile([P, BANK], F32, tag="y_bank", name="y_bank")
@@ -176,25 +174,41 @@ def tile_differentialattention_pa_s_kernel(tc, x, Wq, Wk, lq1, lq2, lk1, lk2, ou
                 else:
                     nc.scalar.activation(out=target, in_=source, func=ACT.Copy, scale=SCALE)
 
+        def transpose_rows(row_words, passes):
+            bank = banks.tile([P, len(passes), 2, P], F32, tag="bank", name="rows_bank")
+            for n, g in enumerate(passes):
+                transpose_words(nc, bank[:, n : n + 1], ident[:], row_words, g)
+            return bank
+
+        def empty_rows(rows, passes, bank, engine):
+            target = rows[:, passes[0] : passes[-1] + 1]
+            source = bank[:].rearrange("p g u r -> p g r u")
+            if engine == "vector":
+                nc.vector.tensor_copy(out=target, in_=source)
+            else:
+                nc.scalar.copy(out=target, in_=source)
+
+        def quantise_rows(rows):
+            codes = row_codes.tile([P, PASSES * P], U32, align_bytes=64, name="codes")
+            scales = row_codes.tile([P, PASSES * P], U8, align_bytes=64, name="scales")
+            nc.vector.quantize_mx(
+                out=codes[:].bitcast(FP8X4),
+                scales=scales[:],
+                in_=rows[:].rearrange("p g r u -> p (g r u)").bitcast(BF16),
+            )
+            return codes, scales
+
+        def new_rows():
+            return row_codes.tile([P, PASSES, P, 2], F32, align_bytes=64, name="rows")
+
         both = ("scalar", "scalar")
         split = ("scalar", "vector")
         transpose_tile(0)
         empty_banks(0, split)
-        x_grouped = keep.tile([P, PASSES, P, 2], F32, align_bytes=64, name="x_grouped")
-        x_bank = banks.tile([P, PASSES, 2, P], F32, tag="bank", name="x_bank")
         x_words = x_sb[:].bitcast(F32).rearrange("r (e g p u) -> r e g u p", e=1, g=PASSES, u=2)
-        for g in range(PASSES):
-            transpose_words(nc, x_bank[:, g : g + 1], ident[:], x_words, g)
-        nc.vector.tensor_copy(
-            out=x_grouped[:], in_=x_bank[:].rearrange("p g u r -> p g r u")
-        )
-        x_codes = keep.tile([P, PASSES * P], U32, align_bytes=64, name="x_codes")
-        x_scales = keep.tile([P, PASSES * P], U8, align_bytes=64, name="x_scales")
-        nc.vector.quantize_mx(
-            out=x_codes[:].bitcast(FP8X4),
-            scales=x_scales[:],
-            in_=x_grouped[:].rearrange("p g r u -> p (g r u)").bitcast(BF16),
-        )
+        x_grouped = new_rows()
+        empty_rows(x_grouped, BOTH_PASSES, transpose_rows(x_words, BOTH_PASSES), "vector")
+        x_codes, x_scales = quantise_rows(x_grouped)
         transpose_tile(1)
         empty_banks(1, both)
         quantise_tile(0)
@@ -229,33 +243,39 @@ def tile_differentialattention_pa_s_kernel(tc, x, Wq, Wk, lq1, lq2, lk1, lk2, ou
         sort_words(7)
         quantise_tile(4)
         unpack(q_rows, HEADS, HEADS, y_q1[:])
-        transpose_tile(7)
-        empty_banks(7, both)
+        last_words = sorted_words[7]
+        last = (new_rows(), new_rows())
+        bank = transpose_rows(last_words[:, 0:1], BOTH_PASSES)
+        empty_rows(last[0], BOTH_PASSES, bank, "scalar")
+        bank_0 = transpose_rows(last_words[:, 1:2], (0,))
+        bank_1 = transpose_rows(last_words[:, 1:2], (1,))
+        empty_rows(last[1], (0,), bank_0, "scalar")
         quantise_tile(5)
         fill_blocks(0, 4, "scalar")
         y_k0 = multiply_pair(4)
         quantise_tile(6)
-        quantise_half(7, 0)
-        quantise_half(7, 1)
+        empty_rows(last[1], (1,), bank_1, "vector")
+        last_codes = [quantise_rows(rows) for rows in last]
         fill_blocks(4, 4, "scalar")
-        y_k = {}
-        for n in (6, 7):
-            y_k[n] = y_pool.tile([P, BANK], F32, tag="y_bank", name="y_bank")
-            multiply_tile(n, y_k[n][:, 0:N_TILE])
+        lam_bank = banks.tile([P, 2], F32, tag="bank", name="lam_bank")
+        nc.tensor.matmul(out=lam_bank[:], lhsT=ones[:], rhs=lam_dots[:], start=True, stop=True)
+        y_k2 = y_pool.tile([P, N_TILE], F32, tag="y_bank", name="y_bank")
+        multiply_tile(6, y_k2[:])
+        y_k3 = y_pool.tile([P, N_TILE], F32, tag="y_bank", name="y_bank")
+        for half in range(2):
+            multiply(*last_codes[half], y_k3[:, half * P : (half + 1) * P])
         unpack(k_rows, 0, HEADS, y_k0[:])
-        for n in (6, 7):
+        for n, y_bank in enumerate((y_k2, y_k3)):
             for half in range(2):
                 unpack(
                     k_rows,
-                    (n - 4) * TILE_ROWS + half * QUADS,
+                    HEADS + n * TILE_ROWS + half * QUADS,
                     QUADS,
-                    y_k[n][:, half * P : (half + 1) * P],
+                    y_bank[:, half * P : (half + 1) * P],
                 )
         fill_blocks(8, 8, "scalar")
         fill_blocks(16, 8, "vector")
 
-        lam_bank = banks.tile([P, 2], F32, tag="bank", name="lam_bank")
-        nc.tensor.matmul(out=lam_bank[:], lhsT=ones[:], rhs=lam_dots[:], start=True, stop=True)
         lam_exp = keep.tile([P, 2], F32, name="lam_exp")
         nc.scalar.activation(out=lam_exp[:], in_=lam_bank[:], func=ACT.Exp)
 
@@ -267,8 +287,8 @@ def tile_differentialattention_pa_s_kernel(tc, x, Wq, Wk, lq1, lq2, lk1, lk2, ou
                 out=idle_bank[:],
                 lhsT=x_codes[:, 0:P].bitcast(FP8X4),
                 lhsT_scale=x_scales[:, 0:P],
-                rhs=w_codes[7][:, 0:N_TILE].bitcast(FP8X4),
-                rhs_scale=w_scales[7][:, 0:N_TILE],
+                rhs=w_codes[6][:, 0:N_TILE].bitcast(FP8X4),
+                rhs_scale=w_scales[6][:, 0:N_TILE],
                 start=True,
                 stop=True,
             )
@@ -290,13 +310,13 @@ def tile_differentialattention_pa_s_kernel(tc, x, Wq, Wk, lq1, lq2, lk1, lk2, ou
                 op=ALU.add,
             )
 
-        def score(ts):
-            bank = banks.tile([P, ts.stop - ts.start, SCORE_COLS], F32, tag="bank", name="scores")
+        def score(ts, cols):
+            bank = banks.tile([P, ts.stop - ts.start, cols], F32, tag="bank", name="scores")
             for t in range(ts.start, ts.stop):
                 nc.tensor.matmul(
                     out=bank[:, t - ts.start, :],
                     lhsT=q_blocks[:, t].rearrange("p c i -> p (c i)"),
-                    rhs=k_rows[:, :, t],
+                    rhs=k_rows[:, 0:cols, t],
                     start=True,
                     stop=True,
                 )
@@ -332,20 +352,21 @@ def tile_differentialattention_pa_s_kernel(tc, x, Wq, Wk, lq1, lq2, lk1, lk2, ou
                 op0=ALU.mult,
                 op1=ALU.add,
             )
-            blocks = (ts.stop - ts.start) // 4
             factor = inverse[:, ts].rearrange("p (b t) -> p b t", t=4)
-            nc.vector.tensor_tensor(
-                out=terms[:, :, ts].rearrange("p h (b t) -> p b h t", t=4),
-                in0=mixed[:, ts].rearrange("p (b t) h -> p b h t", t=4),
-                in1=factor.unsqueeze(2).to_broadcast([P, blocks, HEADS, 4]),
-                op=ALU.mult,
-            )
+            blocks = factor.shape[1]
+            for hs in H_HALVES if ts.stop == QUAD else (slice(0, HEADS),):
+                nc.vector.tensor_tensor(
+                    out=terms[:, hs, ts].rearrange("p h (b t) -> p b h t", t=4),
+                    in0=mixed[:, ts, hs].rearrange("p (b t) h -> p b h t", t=4),
+                    in1=factor.unsqueeze(2).to_broadcast([P, blocks, hs.stop - hs.start, 4]),
+                    op=ALU.mult,
+                )
 
         before = None
-        for size in CHUNK_SIZES:
+        for size, cols in zip(CHUNK_SIZES, SCORE_COLS):
             first_t = 0 if before is None else before.stop
             ts = slice(first_t, first_t + size)
-            exponentiate(ts, score(ts))
+            exponentiate(ts, score(ts, cols))
             if before is None:
                 neg_lam = keep.tile([P, 1], F32, name="neg_lam")
                 nc.vector.scalar_tensor_tensor(
@@ -365,17 +386,20 @@ def tile_differentialattention_pa_s_kernel(tc, x, Wq, Wk, lq1, lq2, lk1, lk2, ou
         normalise(before)
 
         rows_t = keep.tile([P, HEADS, ROWS], F32, align_bytes=64, name="rows_t")
-        nc.vector.transpose(
-            out=rows_t[:].rearrange("p h i -> p (h i)"), in_=terms[:].rearrange("p h t -> p (h t)")
-        )
+        for hs in H_HALVES:
+            nc.vector.transpose(
+                out=rows_t[:, hs].rearrange("p h i -> p (h i)"),
+                in_=terms[:, hs].rearrange("p h t -> p (h t)"),
+            )
         result = keep.tile([P, HEADS, HEADS], F32, name="result")
         by_rows = rows_t[:].rearrange("p h (half b a) -> p half b h a", half=2, a=4)
-        nc.vector.tensor_tensor(
-            out=result[:].rearrange("p (b a) h -> p b h a", a=4),
-            in0=by_rows[:, 0],
-            in1=by_rows[:, 1],
-            op=ALU.add,
-        )
+        for hs in H_HALVES:
+            nc.vector.tensor_tensor(
+                out=result[:, :, hs].rearrange("p (b a) h -> p b h a", a=4),
+                in0=by_rows[:, 0, :, hs],
+                in1=by_rows[:, 1, :, hs],
+                op=ALU.add,
+            )
         nc.sync.dma_start(
             out=out.rearrange("b n a h -> (b n) (a h)"), in_=result[:].rearrange("p a h -> p (a h)")
         )

@@ -33,7 +33,7 @@ CHUNK_SIZES = (8, 8, 8, 4, 4)
 SCALE = D ** -0.5
 LAM_INIT = 0.8 - 0.6 * math.exp(-0.3 * 12)
 H_HALVES = (slice(0, HEADS // 2), slice(HEADS // 2, HEADS))
-BURST = 7
+BURST = 9
 SCORE_COLS = (64, 44, 44, 44, 44)
 
 FLOPS = 2 * P * K * 2 * K + 2 * P * ROWS * ROWS * D
@@ -96,21 +96,12 @@ def tile_differentialattention_pa_s_kernel(tc, x, Wq, Wk, lq1, lq2, lk1, lk2, ou
         w_codes = {}
         w_scales = {}
 
-        sorted_words = {}
-
         def words_of_tile(n):
             words = w_tiles[n][:].rearrange("r e k -> r (e k)").bitcast(F32)
             return words.rearrange("r (e g p u) -> r e g u p", e=2, g=PASSES, u=2)
 
-        def sort_words(n):
-            sorted_words[n] = stage.tile([P, 2, PASSES, 2, P], F32, name="sorted_words")
-            nc.vector.tensor_copy(
-                out=sorted_words[n][:].rearrange("r e g u p -> r (e g) u p"),
-                in_=words_of_tile(n).rearrange("r e g u p -> r (e g) u p"),
-            )
-
         def transpose_tile(n):
-            row_words = sorted_words[n][:] if n in sorted_words else words_of_tile(n)
+            row_words = words_of_tile(n)
             for g in range(PASSES):
                 w_banks[n, g] = banks.tile([P, 2, 2, P], F32, tag="bank", name="w_bank")
                 transpose_words(nc, w_banks[n, g], ident[:], row_words, g)
@@ -202,12 +193,11 @@ def tile_differentialattention_pa_s_kernel(tc, x, Wq, Wk, lq1, lq2, lk1, lk2, ou
             return row_codes.tile([P, PASSES, P, 2], F32, align_bytes=64, name="rows")
 
         both = ("scalar", "scalar")
-        split = ("scalar", "vector")
         transpose_tile(0)
-        empty_banks(0, split)
+        empty_banks(0, both)
         x_words = x_sb[:].bitcast(F32).rearrange("r (e g p u) -> r e g u p", e=1, g=PASSES, u=2)
         x_grouped = new_rows()
-        empty_rows(x_grouped, BOTH_PASSES, transpose_rows(x_words, BOTH_PASSES), "vector")
+        empty_rows(x_grouped, BOTH_PASSES, transpose_rows(x_words, BOTH_PASSES), "scalar")
         x_codes, x_scales = quantise_rows(x_grouped)
         transpose_tile(1)
         empty_banks(1, both)
@@ -227,23 +217,20 @@ def tile_differentialattention_pa_s_kernel(tc, x, Wq, Wk, lq1, lq2, lk1, lk2, ou
         transpose_tile(3)
         empty_banks(3, both)
         y_q0 = multiply_pair(0)
-        sort_words(4)
         quantise_tile(2)
         transpose_tile(4)
         empty_banks(4, both)
-        sort_words(5)
         unpack(q_rows, 0, HEADS, y_q0[:])
         transpose_tile(5)
         empty_banks(5, both)
         quantise_tile(3)
-        sort_words(6)
         y_q1 = multiply_pair(2)
         transpose_tile(6)
         empty_banks(6, both)
-        sort_words(7)
         quantise_tile(4)
         unpack(q_rows, HEADS, HEADS, y_q1[:])
-        last_words = sorted_words[7]
+
+        last_words = words_of_tile(7)
         last = (new_rows(), new_rows())
         bank = transpose_rows(last_words[:, 0:1], BOTH_PASSES)
         empty_rows(last[0], BOTH_PASSES, bank, "scalar")

@@ -33,8 +33,8 @@ CHUNK_SIZES = (8, 8, 8, 4, 4)
 SCALE = D ** -0.5
 LAM_INIT = 0.8 - 0.6 * math.exp(-0.3 * 12)
 H_HALVES = (slice(0, HEADS // 2), slice(HEADS // 2, HEADS))
-BURST = 9
-SCORE_COLS = (64, 44, 44, 44, 44)
+BURST = 6
+SCORE_COLS = 50
 
 FLOPS = 2 * P * K * 2 * K + 2 * P * ROWS * ROWS * D
 
@@ -88,7 +88,7 @@ def tile_differentialattention_pa_s_kernel(tc, x, Wq, Wk, lq1, lq2, lk1, lk2, ou
         nc.vector.memset(q_blocks[:, 0 : QUAD // 2], 0.0)
         nc.gpsimd.memset(q_blocks[:, QUAD // 2 : QUAD], 0.0)
         q_rows = keep.tile([P, ROWS, QUAD], F32, align_bytes=64, name="q_rows")
-        k_rows = keep.tile([P, max(SCORE_COLS), QUAD], F32, align_bytes=64, name="k_rows")
+        k_rows = keep.tile([P, SCORE_COLS, QUAD], F32, align_bytes=64, name="k_rows")
         nc.gpsimd.memset(k_rows[:, ROWS:, :], 0.0)
 
         w_banks = {}
@@ -297,13 +297,13 @@ def tile_differentialattention_pa_s_kernel(tc, x, Wq, Wk, lq1, lq2, lk1, lk2, ou
                 op=ALU.add,
             )
 
-        def score(ts, cols):
-            bank = banks.tile([P, ts.stop - ts.start, cols], F32, tag="bank", name="scores")
+        def score(ts):
+            bank = banks.tile([P, ts.stop - ts.start, SCORE_COLS], F32, tag="bank", name="scores")
             for t in range(ts.start, ts.stop):
                 nc.tensor.matmul(
                     out=bank[:, t - ts.start, :],
                     lhsT=q_blocks[:, t].rearrange("p c i -> p (c i)"),
-                    rhs=k_rows[:, 0:cols, t],
+                    rhs=k_rows[:, :, t],
                     start=True,
                     stop=True,
                 )
@@ -350,10 +350,10 @@ def tile_differentialattention_pa_s_kernel(tc, x, Wq, Wk, lq1, lq2, lk1, lk2, ou
                 )
 
         before = None
-        for size, cols in zip(CHUNK_SIZES, SCORE_COLS):
+        for size in CHUNK_SIZES:
             first_t = 0 if before is None else before.stop
             ts = slice(first_t, first_t + size)
-            exponentiate(ts, score(ts, cols))
+            exponentiate(ts, score(ts))
             if before is None:
                 neg_lam = keep.tile([P, 1], F32, name="neg_lam")
                 nc.vector.scalar_tensor_tensor(

@@ -33,8 +33,8 @@ CHUNK_SIZES = (8, 8, 8, 4, 4)
 SCALE = D ** -0.5
 LAM_INIT = 0.8 - 0.6 * math.exp(-0.3 * 12)
 H_HALVES = (slice(0, HEADS // 2), slice(HEADS // 2, HEADS))
-BURST = 6
-SCORE_COLS = 50
+BURST = 7
+SCORE_COLS = 48
 
 FLOPS = 2 * P * K * 2 * K + 2 * P * ROWS * ROWS * D
 
@@ -194,10 +194,10 @@ def tile_differentialattention_pa_s_kernel(tc, x, Wq, Wk, lq1, lq2, lk1, lk2, ou
 
         both = ("scalar", "scalar")
         transpose_tile(0)
-        empty_banks(0, both)
+        empty_banks(0, ("scalar", "vector"))
         x_words = x_sb[:].bitcast(F32).rearrange("r (e g p u) -> r e g u p", e=1, g=PASSES, u=2)
         x_grouped = new_rows()
-        empty_rows(x_grouped, BOTH_PASSES, transpose_rows(x_words, BOTH_PASSES), "scalar")
+        empty_rows(x_grouped, BOTH_PASSES, transpose_rows(x_words, BOTH_PASSES), "vector")
         x_codes, x_scales = quantise_rows(x_grouped)
         transpose_tile(1)
         empty_banks(1, both)
@@ -260,7 +260,7 @@ def tile_differentialattention_pa_s_kernel(tc, x, Wq, Wk, lq1, lq2, lk1, lk2, ou
                     QUADS,
                     y_bank[:, half * P : (half + 1) * P],
                 )
-        fill_blocks(8, 8, "scalar")
+        fill_blocks(8, 8, "vector")
         fill_blocks(16, 8, "vector")
 
         lam_exp = keep.tile([P, 2], F32, name="lam_exp")

@@ -73,7 +73,7 @@ def tile_differentialattention_pa_s_kernel(tc, x, Wq, Wk, lq1, lq2, lk1, lk2, ou
         lam_rows = keep.tile([P, 4 * D], BF16, name="lam_rows")
         nc.vector.memset(lam_rows[:], 0.0)
         for n, vector in enumerate((lq1, lq2, lk1, lk2)):
-            nc.scalar.dma_start(
+            nc.sync.dma_start(
                 out=lam_rows[0:1, n * D : (n + 1) * D], in_=vector.rearrange("(o d) -> o d", o=1)
             )
 
@@ -202,15 +202,6 @@ def tile_differentialattention_pa_s_kernel(tc, x, Wq, Wk, lq1, lq2, lk1, lk2, ou
         transpose_tile(1)
         empty_banks(1, both)
         quantise_tile(0)
-        lam_prod = keep.tile([P, 2, D], F32, name="lam_prod")
-        nc.vector.tensor_tensor(
-            out=lam_prod[:].rearrange("p n d -> p (n d)"),
-            in0=lam_rows[:, 0 : 2 * D],
-            in1=lam_rows[:, 2 * D : 4 * D],
-            op=ALU.mult,
-        )
-        lam_dots = keep.tile([P, 2], F32, name="lam_dots")
-        nc.vector.tensor_reduce(out=lam_dots[:], in_=lam_prod[:], axis=AXIS.X, op=ALU.add)
         transpose_tile(2)
         empty_banks(2, both)
         quantise_tile(1)
@@ -244,8 +235,10 @@ def tile_differentialattention_pa_s_kernel(tc, x, Wq, Wk, lq1, lq2, lk1, lk2, ou
         empty_rows(last[1], (1,), bank_1, "vector")
         last_codes = [quantise_rows(rows) for rows in last]
         fill_blocks(4, 4, "scalar")
-        lam_bank = banks.tile([P, 2], F32, tag="bank", name="lam_bank")
-        nc.tensor.matmul(out=lam_bank[:], lhsT=ones[:], rhs=lam_dots[:], start=True, stop=True)
+        lam_prod = keep.tile([P, 2 * D], F32, name="lam_prod")
+        nc.gpsimd.tensor_tensor(
+            out=lam_prod[:], in0=lam_rows[:, 0 : 2 * D], in1=lam_rows[:, 2 * D : 4 * D], op=ALU.mult
+        )
         y_k2 = y_pool.tile([P, N_TILE], F32, tag="y_bank", name="y_bank")
         multiply_tile(6, y_k2[:])
         y_k3 = y_pool.tile([P, N_TILE], F32, tag="y_bank", name="y_bank")
@@ -263,8 +256,8 @@ def tile_differentialattention_pa_s_kernel(tc, x, Wq, Wk, lq1, lq2, lk1, lk2, ou
         fill_blocks(8, 8, "vector")
         fill_blocks(16, 8, "vector")
 
-        lam_exp = keep.tile([P, 2], F32, name="lam_exp")
-        nc.scalar.activation(out=lam_exp[:], in_=lam_bank[:], func=ACT.Exp)
+        lam_bank = banks.tile([P, 2 * D], F32, tag="bank", name="lam_bank")
+        nc.tensor.matmul(out=lam_bank[:], lhsT=ones[:], rhs=lam_prod[:], start=True, stop=True)
 
         fill_blocks(24, 8, "scalar")
 
@@ -355,6 +348,15 @@ def tile_differentialattention_pa_s_kernel(tc, x, Wq, Wk, lq1, lq2, lk1, lk2, ou
             ts = slice(first_t, first_t + size)
             exponentiate(ts, score(ts))
             if before is None:
+                lam_dots = keep.tile([P, 2], F32, name="lam_dots")
+                nc.vector.tensor_reduce(
+                    out=lam_dots[:],
+                    in_=lam_bank[:].rearrange("p (n d) -> p n d", n=2),
+                    axis=AXIS.X,
+                    op=ALU.add,
+                )
+                lam_exp = keep.tile([P, 2], F32, name="lam_exp")
+                nc.scalar.activation(out=lam_exp[:], in_=lam_dots[:], func=ACT.Exp)
                 neg_lam = keep.tile([P, 1], F32, name="neg_lam")
                 nc.vector.scalar_tensor_tensor(
                     out=neg_lam[:],

@@ -100,8 +100,17 @@ def tile_differentialattention_pa_s_kernel(tc, x, Wq, Wk, lq1, lq2, lk1, lk2, ou
             words = w_tiles[n][:].rearrange("r e k -> r (e k)").bitcast(F32)
             return words.rearrange("r (e g p u) -> r e g u p", e=2, g=PASSES, u=2)
 
+        sorted_words = {}
+
+        def sort_words(n):
+            sorted_words[n] = stage.tile([P, 2, PASSES, 2, P], F32, name="sorted_words")
+            nc.vector.tensor_copy(
+                out=sorted_words[n][:].rearrange("r e g u p -> r (e g) u p"),
+                in_=words_of_tile(n).rearrange("r e g u p -> r (e g) u p"),
+            )
+
         def transpose_tile(n):
-            row_words = words_of_tile(n)
+            row_words = sorted_words[n][:] if n in sorted_words else words_of_tile(n)
             for g in range(PASSES):
                 w_banks[n, g] = banks.tile([P, 2, 2, P], F32, tag="bank", name="w_bank")
                 transpose_words(nc, w_banks[n, g], ident[:], row_words, g)
@@ -208,6 +217,7 @@ def tile_differentialattention_pa_s_kernel(tc, x, Wq, Wk, lq1, lq2, lk1, lk2, ou
         transpose_tile(3)
         empty_banks(3, both)
         y_q0 = multiply_pair(0)
+        sort_words(4)
         quantise_tile(2)
         transpose_tile(4)
         empty_banks(4, both)
@@ -215,6 +225,7 @@ def tile_differentialattention_pa_s_kernel(tc, x, Wq, Wk, lq1, lq2, lk1, lk2, ou
         transpose_tile(5)
         empty_banks(5, both)
         quantise_tile(3)
+        sort_words(6)
         y_q1 = multiply_pair(2)
         transpose_tile(6)
         empty_banks(6, both)

from contextlib import ExitStack
import math

import concourse.mybir as mybir
from concourse.masks import make_identity

F32 = mybir.dt.float32
BF16 = mybir.dt.bfloat16
U32 = mybir.dt.uint32
U8 = mybir.dt.uint8
I32 = mybir.dt.int32
FP8X4 = mybir.dt.float8_e4m3fn_x4
ALU = mybir.AluOpType
ACT = mybir.ActivationFunctionType
AXIS = mybir.AxisListType

P = 128
K = 1024
K_PASS = 512
PASSES = K // K_PASS
WORDS = K // 2
HEADS = 16
ROWS = 2 * HEADS
D = 32
QUAD = 32
QUADS = P // QUAD
BOTH_PASSES = tuple(range(PASSES))
BANK = 512
W_TILES = 4
TILE_ROWS = 8
N_TILE = TILE_ROWS * D
CHUNK_SIZES = (8, 8, 8, 4, 4)
SCALE = D ** -0.5
LAM_INIT = 0.8 - 0.6 * math.exp(-0.3 * 12)
H_HALVES = (slice(0, HEADS // 2), slice(HEADS // 2, HEADS))
BURST = 7
SCORE_COLS = 48

FLOPS = 2 * P * K * 2 * K + 2 * P * ROWS * ROWS * D


def transpose_words(nc, bank, ident, row_words, g):
    for e in range(row_words.shape[1]):
        for u in range(2):
            nc.tensor.transpose(bank[:, e, u, :], row_words[:, e, g, u, :], ident)


def tile_differentialattention_pa_s_kernel(tc, x, Wq, Wk, lq1, lq2, lk1, lk2, out):
    nc = tc.nc
    with ExitStack() as ctx:
        keep = ctx.enter_context(tc.tile_pool(name="keep", bufs=1))
        stage = ctx.enter_context(tc.tile_pool(name="stage", bufs=4))
        row_codes = ctx.enter_context(tc.tile_pool(name="row_codes", bufs=3))
        banks = ctx.enter_context(tc.psum_pool(name="banks", bufs=5))
        y_pool = ctx.enter_context(tc.psum_pool(name="y_pool", bufs=3))
        ctx.enter_context(tc.manual_schedule())

        x_sb = keep.tile([P, K], BF16, name="x_sb")
        w_tiles = []
        for w in (Wq, Wk):
            w_view = w.rearrange("(s e p j) k -> j s p e k", s=2, e=2, j=2)
            for j in range(2):
                for s in range(2):
                    w_sb = keep.tile([P, 2, K], BF16, name="w_sb%d" % len(w_tiles))
                    if not w_tiles:
                        for e in range(2):
                            nc.sync.dma_start(out=w_sb[:, e], in_=w_view[j, s, :, e])
                        nc.sync.dma_start(out=x_sb[:], in_=x.rearrange("b n k -> (b n) k"))
                    else:
                        nc.sync.dma_start(out=w_sb[:], in_=w_view[j, s])
                    w_tiles.append(w_sb)

        lam_rows = keep.tile([P, 4 * D], BF16, name="lam_rows")
        nc.vector.memset(lam_rows[:], 0.0)
        for n, vector in enumerate((lq1, lq2, lk1, lk2)):
            nc.sync.dma_start(
                out=lam_rows[0:1, n * D : (n + 1) * D], in_=vector.rearrange("(o d) -> o d", o=1)
            )

        ident = keep.tile([P, P], F32, name="ident")
        make_identity(nc, ident[:])
        ones = keep.tile([P, P], F32, name="ones")
        nc.vector.memset(ones[:], 1.0)
        warm = keep.tile([P, 2], F32, name="warm")
        nc.vector.memset(warm[:], 0.0)
        nc.scalar.activation(out=warm[:, 1:2], in_=warm[:, 0:1], func=ACT.Exp)
        q_blocks = keep.tile([P, QUAD, QUADS, ROWS], F32, name="q_blocks")
        nc.vector.memset(q_blocks[:, 0 : QUAD // 2], 0.0)
        nc.gpsimd.memset(q_blocks[:, QUAD // 2 : QUAD], 0.0)
        q_rows = keep.tile([P, ROWS, QUAD], F32, align_bytes=64, name="q_rows")
        k_rows = keep.tile([P, SCORE_COLS, QUAD], F32, align_bytes=64, name="k_rows")
        nc.gpsimd.memset(k_rows[:, ROWS:, :], 0.0)

        w_banks = {}
        grouped = {}
        w_codes = {}
        w_scales = {}

        def words_of_tile(n):
            words = w_tiles[n][:].rearrange("r e k -> r (e k)").bitcast(F32)
            return words.rearrange("r (e g p u) -> r e g u p", e=2, g=PASSES, u=2)

        sorted_words = {}

        def sort_words(n):
            sorted_words[n] = stage.tile([P, 2, PASSES, 2, P], F32, name="sorted_words")
            nc.vector.tensor_copy(
                out=sorted_words[n][:].rearrange("r e g u p -> r (e g) u p"),
                in_=words_of_tile(n).rearrange("r e g u p -> r (e g) u p"),
            )

        def transpose_tile(n):
            row_words = sorted_words[n][:] if n in sorted_words else words_of_tile(n)
            for g in range(PASSES):
                w_banks[n, g] = banks.tile([P, 2, 2, P], F32, tag="bank", name="w_bank")
                transpose_words(nc, w_banks[n, g], ident[:], row_words, g)

        def empty_banks(n, engines):
            grouped[n] = stage.tile([P, PASSES, 2, P, 2], F32, align_bytes=64, name="grouped")
            for g in range(PASSES):
                source = w_banks[n, g][:].rearrange("p e u r -> p e r u")
                if engines[g] == "vector":
                    nc.vector.tensor_copy(out=grouped[n][:, g], in_=source)
                else:
                    nc.scalar.copy(out=grouped[n][:, g], in_=source)

        def quantise_tile(n):
            w_codes[n] = stage.tile([P, PASSES * N_TILE], U32, align_bytes=64, name="w_codes")
            w_scales[n] = stage.tile([P, PASSES * N_TILE], U8, align_bytes=64, name="w_scales")
            nc.vector.quantize_mx(
                out=w_codes[n][:].bitcast(FP8X4),
                scales=w_scales[n][:],
                in_=grouped[n][:].rearrange("p g e r u -> p (g e r u)").bitcast(BF16),
            )

        def multiply(codes, scales, y_cols):
            width = y_cols.shape[1]
            for g in range(PASSES):
                x_cols = slice(g * P, (g + 1) * P)
                w_cols = slice(g * width, (g + 1) * width)
                nc.tensor.matmul_mx(
                    out=y_cols,
                    lhsT=x_codes[:, x_cols].bitcast(FP8X4),
                    lhsT_scale=x_scales[:, x_cols],
                    rhs=codes[:, w_cols].bitcast(FP8X4),
                    rhs_scale=scales[:, w_cols],
                    start=(g == 0),
                    stop=(g == PASSES - 1),
                )

        def multiply_tile(n, y_cols):
            multiply(w_codes[n], w_scales[n], y_cols)

        def multiply_pair(n):
            y_bank = y_pool.tile([P, BANK], F32, tag="y_bank", name="y_bank")
            multiply_tile(n, y_bank[:, 0:N_TILE])
            multiply_tile(n + 1, y_bank[:, N_TILE : 2 * N_TILE])
            return y_bank

        def unpack(rows_tile, first_row, rows, y_cols):
            target = rows_tile[:, first_row : first_row + rows, :].rearrange("p i t -> p (i t)")
            nc.vector.transpose(out=target, in_=y_cols)

        def fill_blocks(first_t, tokens, engine):
            ts = slice(first_t, first_t + tokens)
            for c in range(QUADS):
                rows = slice(c * QUAD, (c + 1) * QUAD)
                target = q_blocks[rows, ts, c, :].rearrange("p t (b i) -> p b t i", i=4)
                source = q_rows[rows, :, ts].rearrange("p (b i) t -> p b t i", i=4)
                if engine == "vector":
                    nc.vector.tensor_scalar(
                        out=target, in0=source, scalar1=SCALE, scalar2=None, op0=ALU.mult
                    )
                else:
                    nc.scalar.activation(out=target, in_=source, func=ACT.Copy, scale=SCALE)

        def transpose_rows(row_words, passes):
            bank = banks.tile([P, len(passes), 2, P], F32, tag="bank", name="rows_bank")
            for n, g in enumerate(passes):
                transpose_words(nc, bank[:, n : n + 1], ident[:], row_words, g)
            return bank

        def empty_rows(rows, passes, bank, engine):
            target = rows[:, passes[0] : passes[-1] + 1]
            source = bank[:].rearrange("p g u r -> p g r u")
            if engine == "vector":
                nc.vector.tensor_copy(out=target, in_=source)
            else:
                nc.scalar.copy(out=target, in_=source)

        def quantise_rows(rows):
            codes = row_codes.tile([P, PASSES * P], U32, align_bytes=64, name="codes")
            scales = row_codes.tile([P, PASSES * P], U8, align_bytes=64, name="scales")
            nc.vector.quantize_mx(
                out=codes[:].bitcast(FP8X4),
                scales=scales[:],
                in_=rows[:].rearrange("p g r u -> p (g r u)").bitcast(BF16),
            )
            return codes, scales

        def new_rows():
            return row_codes.tile([P, PASSES, P, 2], F32, align_bytes=64, name="rows")

        both = ("scalar", "scalar")
        transpose_tile(0)
        empty_banks(0, ("scalar", "vector"))
        x_words = x_sb[:].bitcast(F32).rearrange("r (e g p u) -> r e g u p", e=1, g=PASSES, u=2)
        x_grouped = new_rows()
        empty_rows(x_grouped, BOTH_PASSES, transpose_rows(x_words, BOTH_PASSES), "vector")
        x_codes, x_scales = quantise_rows(x_grouped)
        transpose_tile(1)
        empty_banks(1, both)
        quantise_tile(0)
        transpose_tile(2)
        empty_banks(2, both)
        quantise_tile(1)
        transpose_tile(3)
        empty_banks(3, both)
        y_q0 = multiply_pair(0)
        sort_words(4)
        quantise_tile(2)
        transpose_tile(4)
        empty_banks(4, both)
        unpack(q_rows, 0, HEADS, y_q0[:])
        transpose_tile(5)
        empty_banks(5, both)
        quantise_tile(3)
        sort_words(6)
        y_q1 = multiply_pair(2)
        transpose_tile(6)
        empty_banks(6, both)
        quantise_tile(4)
        unpack(q_rows, HEADS, HEADS, y_q1[:])

        last_words = words_of_tile(7)
        last = (new_rows(), new_rows())
        bank = transpose_rows(last_words[:, 0:1], BOTH_PASSES)
        empty_rows(last[0], BOTH_PASSES, bank, "scalar")
        bank_0 = transpose_rows(last_words[:, 1:2], (0,))
        bank_1 = transpose_rows(last_words[:, 1:2], (1,))
        empty_rows(last[1], (0,), bank_0, "scalar")
        quantise_tile(5)
        fill_blocks(0, 4, "scalar")
        y_k0 = multiply_pair(4)
        quantise_tile(6)
        empty_rows(last[1], (1,), bank_1, "vector")
        last_codes = [quantise_rows(rows) for rows in last]
        fill_blocks(4, 4, "scalar")
        lam_prod = keep.tile([P, 2 * D], F32, name="lam_prod")
        nc.gpsimd.tensor_tensor(
            out=lam_prod[:], in0=lam_rows[:, 0 : 2 * D], in1=lam_rows[:, 2 * D : 4 * D], op=ALU.mult
        )
        y_k2 = y_pool.tile([P, N_TILE], F32, tag="y_bank", name="y_bank")
        multiply_tile(6, y_k2[:])
        y_k3 = y_pool.tile([P, N_TILE], F32, tag="y_bank", name="y_bank")
        for half in range(2):
            multiply(*last_codes[half], y_k3[:, half * P : (half + 1) * P])
        unpack(k_rows, 0, HEADS, y_k0[:])
        for n, y_bank in enumerate((y_k2, y_k3)):
            for half in range(2):
                unpack(
                    k_rows,
                    HEADS + n * TILE_ROWS + half * QUADS,
                    QUADS,
                    y_bank[:, half * P : (half + 1) * P],
                )
        fill_blocks(8, 8, "vector")
        fill_blocks(16, 8, "vector")

        lam_bank = banks.tile([P, 2 * D], F32, tag="bank", name="lam_bank")
        nc.tensor.matmul(out=lam_bank[:], lhsT=ones[:], rhs=lam_prod[:], start=True, stop=True)

        fill_blocks(24, 8, "scalar")

        idle_bank = banks.tile([P, N_TILE], F32, tag="bank", name="idle_bank")
        for repeat in range(BURST):
            nc.tensor.matmul_mx(
                out=idle_bank[:],
                lhsT=x_codes[:, 0:P].bitcast(FP8X4),
                lhsT_scale=x_scales[:, 0:P],
                rhs=w_codes[6][:, 0:N_TILE].bitcast(FP8X4),
                rhs_scale=w_scales[6][:, 0:N_TILE],
                start=True,
                stop=True,
            )

        neg_top = keep.tile([P, QUAD], F32, name="neg_top")
        expd = keep.tile([P, QUAD, ROWS], F32, name="expd")
        sums = keep.tile([P, QUAD], F32, name="sums")
        inverse = keep.tile([P, QUAD], F32, name="inverse")
        mixed = keep.tile([P, QUAD, HEADS], F32, name="mixed")
        terms = keep.tile([P, HEADS, QUAD], F32, align_bytes=64, name="terms")
        half_weights = keep.tile([P, 2], F32, name="half_weights")

        ident_halves = ident[:].rearrange("p (c half i) -> p half c i", c=QUADS, half=2)
        for half in range(2):
            nc.vector.tensor_reduce(
                out=half_weights[:, half : half + 1],
                in_=ident_halves[:, half],
                axis=AXIS.XY,
                op=ALU.add,
            )

        def score(ts):
            bank = banks.tile([P, ts.stop - ts.start, SCORE_COLS], F32, tag="bank", name="scores")
            for t in range(ts.start, ts.stop):
                nc.tensor.matmul(
                    out=bank[:, t - ts.start, :],
                    lhsT=q_blocks[:, t].rearrange("p c i -> p (c i)"),
                    rhs=k_rows[:, :, t],
                    start=True,
                    stop=True,
                )
            return bank

        def exponentiate(ts, bank):
            nc.vector.tensor_reduce(
                out=neg_top[:, ts], in_=bank[:, :, 0:ROWS], axis=AXIS.X, op=ALU.max, negate=True
            )
            for t in range(ts.start, ts.stop):
                nc.scalar.activation(
                    out=expd[:, t, :],
                    in_=bank[:, t - ts.start, 0:ROWS],
                    func=ACT.Exp,
                    bias=neg_top[:, t : t + 1],
                    accum_out=sums[:, t : t + 1],
                )

        def normalise(ts):
            nc.vector.tensor_scalar(
                out=mixed[:, ts],
                in0=expd[:, ts, 0:HEADS],
                scalar1=half_weights[:, 0:1],
                scalar2=None,
                op0=ALU.mult,
            )
            nc.vector.reciprocal(out=inverse[:, ts], in_=sums[:, ts])
            nc.vector.scalar_tensor_tensor(
                out=mixed[:, ts],
                in0=expd[:, ts, HEADS:ROWS],
                scalar=half_weights[:, 1:2],
                in1=mixed[:, ts],
                op0=ALU.mult,
                op1=ALU.add,
            )
            factor = inverse[:, ts].rearrange("p (b t) -> p b t", t=4)
            blocks = factor.shape[1]
            for hs in H_HALVES if ts.stop == QUAD else (slice(0, HEADS),):
                nc.vector.tensor_tensor(
                    out=terms[:, hs, ts].rearrange("p h (b t) -> p b h t", t=4),
                    in0=mixed[:, ts, hs].rearrange("p (b t) h -> p b h t", t=4),
                    in1=factor.unsqueeze(2).to_broadcast([P, blocks, hs.stop - hs.start, 4]),
                    op=ALU.mult,
                )

        before = None
        for size in CHUNK_SIZES:
            first_t = 0 if before is None else before.stop
            ts = slice(first_t, first_t + size)
            exponentiate(ts, score(ts))
            if before is None:
                lam_dots = keep.tile([P, 2], F32, name="lam_dots")
                nc.vector.tensor_reduce(
                    out=lam_dots[:],
                    in_=lam_bank[:].rearrange("p (n d) -> p n d", n=2),
                    axis=AXIS.X,
                    op=ALU.add,
                )
                lam_exp = keep.tile([P, 2], F32, name="lam_exp")
                nc.scalar.activation(out=lam_exp[:], in_=lam_dots[:], func=ACT.Exp)
                neg_lam = keep.tile([P, 1], F32, name="neg_lam")
                nc.vector.scalar_tensor_tensor(
                    out=neg_lam[:],
                    in0=lam_exp[:, 1:2],
                    scalar=-LAM_INIT,
                    in1=lam_exp[:, 0:1],
                    op0=ALU.add,
                    op1=ALU.subtract,
                )
                nc.vector.tensor_tensor(
                    out=half_weights[:, 1:2], in0=half_weights[:, 1:2], in1=neg_lam[:], op=ALU.mult
                )
            else:
                normalise(before)
            before = ts
        normalise(before)

        rows_t = keep.tile([P, HEADS, ROWS], F32, align_bytes=64, name="rows_t")
        for hs in H_HALVES:
            nc.vector.transpose(
                out=rows_t[:, hs].rearrange("p h i -> p (h i)"),
                in_=terms[:, hs].rearrange("p h t -> p (h t)"),
            )
        result = keep.tile([P, HEADS, HEADS], F32, name="result")
        by_rows = rows_t[:].rearrange("p h (half b a) -> p half b h a", half=2, a=4)
        for hs in H_HALVES:
            nc.vector.tensor_tensor(
                out=result[:, :, hs].rearrange("p (b a) h -> p b h a", a=4),
                in0=by_rows[:, 0, :, hs],
                in1=by_rows[:, 1, :, hs],
                op=ALU.add,
            )
        nc.sync.dma_start(
            out=out.rearrange("b n a h -> (b n) (a h)"), in_=result[:].rearrange("p a h -> p (a h)")
        )
